import numpy as np
import ml_dtypes


def mxq(x, axis, fmt="e4m3"):
    dtype, down = {"e4m3": (ml_dtypes.float8_e4m3fn, 7), "e5m2": (ml_dtypes.float8_e5m2, 14)}[fmt]
    v = np.moveaxis(np.asarray(x, np.float32).astype(ml_dtypes.bfloat16).astype(np.float64), axis, -1)
    blocks = v.reshape(v.shape[:-1] + (-1, 32))
    amax = np.abs(blocks).max(-1, keepdims=True)
    byte = np.maximum(np.where(amax > 0, np.frexp(amax)[1] - 1 + 127, 0) - down, 1)
    scale = np.exp2(byte - 127.0)
    codes = (blocks / scale).astype(np.float32).astype(dtype).astype(np.float64)
    return np.moveaxis((codes * scale).reshape(v.shape), -1, axis)


WIDE = False


def mx_kscale(k):
    if not WIDE:
        return np.ones(k)
    levels = np.array([10, -10, 5, -5, 0])
    if k % 512:
        return np.exp2(np.random.permutation(np.resize(levels, k // 32))).repeat(32)
    a = np.empty((k // 512, 16))
    for p in range(k // 512):
        a[p, :8] = np.random.permutation(np.resize(levels, 8))
        for g in range(8):
            far = levels[np.abs(levels - a[p, g]) >= 10]
            a[p, g + 8] = far[np.random.randint(len(far))]
    return np.exp2(a.ravel()).repeat(32)


BF16 = ml_dtypes.bfloat16


def bf(x):
    return np.asarray(x, np.float32).astype(BF16)


def f64(x):
    return np.asarray(x).astype(np.float64)


B, T, C, H, G = 2, 2048, 512, 8, 16
HS = C // H
TG = T // G
THETA = 10000.0


def apply_rope(t, cos, sin):
    tp = t.reshape(B, T, H, HS // 2, 2)
    a, b = tp[..., 0], tp[..., 1]
    c = cos[None, :, None, :]
    s = sin[None, :, None, :]
    return np.stack([a * c - b * s, a * s + b * c], axis=-1).reshape(B, T, H, HS)


def grp(t):
    return t.reshape(B, G, TG, H, HS).transpose(0, 3, 1, 2, 4)


def with_summary(t):
    return np.concatenate([t, t.mean(axis=3, keepdims=True)], axis=3)


def setup_inputs():
    s = mx_kscale(C)
    x = np.random.standard_normal((B, T, C)) * 0.7 + np.random.standard_normal((B, 1, C)) * 0.7
    w = np.random.standard_normal((3 * C, C)) / np.sqrt(C)
    ang = np.arange(T)[:, None] / THETA ** (np.arange(0, HS, 2) / HS)[None, :]
    return {"x": bf(x * s), "w_attn": bf(w / s[None, :]), "freqs_cos": bf(np.cos(ang)), "freqs_sin": bf(np.sin(ang))}


def reference(x, w_attn, freqs_cos, freqs_sin):
    cos, sin = f64(freqs_cos), f64(freqs_sin)
    qkv = mxq(f64(x), 2, "e4m3") @ mxq(f64(w_attn), 1, "e4m3").T
    q, k, v = np.split(qkv, 3, axis=2)
    q = apply_rope(q.reshape(B, T, H, HS), cos, sin).reshape(B, T, C)
    k = apply_rope(k.reshape(B, T, H, HS), cos, sin).reshape(B, T, C)
    q, k, v = grp(q), grp(k), grp(v)
    return with_summary(q), with_summary(k), with_summary(v)

@@ -1,0 +1,374 @@
+from contextlib import ExitStack
+
+import concourse.mybir as mybir
+from concourse.masks import make_identity
+
+F32 = mybir.dt.float32
+BF16 = mybir.dt.bfloat16
+U32 = mybir.dt.uint32
+U8 = mybir.dt.uint8
+FP8X4 = mybir.dt.float8_e4m3fn_x4
+ADD = mybir.AluOpType.add
+MULT = mybir.AluOpType.mult
+COPY = mybir.ActivationFunctionType.Copy
+LAST_AXIS = mybir.AxisListType.X
+
+P = 128
+B, T, C, H, G = 2, 2048, 512, 8, 16
+HS = C // H
+NI = HS // 2
+TG = T // G
+J = 4
+GS = P * J // TG
+NQ = T // (P * J)
+NSPAN = B * NQ
+WORDS = C // 2
+PLANES = WORDS // P
+PACK = 4
+SETS = 4
+HEADS_OF_TILE = 4
+Q_, K_, V_ = 0, 1, 2
+BEATS = 4
+SUM_TILES = 4
+SUM_LAG = 5
+FLOPS = 2 * B * T * 3 * C * C
+
+
+def tile_causalselfattention2_pa_t_kernel(tc, x, w_attn, freqs_cos, freqs_sin, out_0, out_1, out_2):
+    nc = tc.nc
+    outs = [out_0, out_1, out_2]
+    with ExitStack() as ctx:
+        const = ctx.enter_context(tc.tile_pool(name="const", bufs=1))
+        x_pool = ctx.enter_context(tc.tile_pool(name="x_pool", bufs=NSPAN))
+        stage = ctx.enter_context(tc.tile_pool(name="stage", bufs=2))
+        products = ctx.enter_context(tc.tile_pool(name="products", bufs=4))
+        chunk_pool = ctx.enter_context(tc.tile_pool(name="chunk_pool", bufs=7))
+        small = ctx.enter_context(tc.tile_pool(name="small", bufs=2))
+        ps_words = ctx.enter_context(tc.psum_pool(name="ps_words", bufs=1))
+        ps_pass = ctx.enter_context(tc.psum_pool(name="ps_pass", bufs=4))
+        ps_vt = ctx.enter_context(tc.psum_pool(name="ps_vt", bufs=1))
+        ps_sums = ctx.enter_context(tc.psum_pool(name="ps_sums", bufs=2))
+        ctx.enter_context(tc.manual_schedule())
+
+        w_rows = const.tile([P, 3 * SETS, C], BF16)
+        w_view = w_attn.rearrange("(r p) k -> p r k", p=P)
+        x_rows = []
+        for span in range(NSPAN):
+            x_span = x_pool.tile([P, J * C], BF16, name="x_span")
+            x_rows.append(x_span)
+
+        def load_w(t):
+            nc.sync.dma_start(out=w_rows[:, SETS * t : SETS * (t + 1), :], in_=w_view[:, SETS * t : SETS * (t + 1), :])
+
+        def load_x(span):
+            b, qt = divmod(span, NQ)
+            nc.sync.dma_start(
+                out=x_rows[span][:],
+                in_=x[b, qt * P * J : (qt + 1) * P * J, :].rearrange("(p j) k -> p (j k)", j=J),
+            )
+
+        load_w(Q_)
+        load_x(0)
+        load_w(K_)
+        load_w(V_)
+        for span in range(1, NSPAN):
+            load_x(span)
+
+        cos_t = const.tile([P, NQ, J * NI], BF16)
+        sin_t = const.tile([P, NQ, J * NI], BF16)
+        cos_view = freqs_cos.rearrange("(q g n j) i -> g n q (j i)", q=NQ, g=GS, j=J)
+        sin_view = freqs_sin.rearrange("(q g n j) i -> g n q (j i)", q=NQ, g=GS, j=J)
+        for g in range(GS):
+            nc.scalar.dma_start(out=cos_t[g:P:GS, :, :], in_=cos_view[g])
+            nc.scalar.dma_start(out=sin_t[g:P:GS, :, :], in_=sin_view[g])
+
+        ident = const.tile([P, P], F32)
+        make_identity(nc, ident[:])
+        spread = const.tile([P, P], F32)
+        nc.vector.tensor_copy(
+            out=spread[:].rearrange("k (n g) -> k n g", g=GS),
+            in_=ident[:].rearrange("k (g n) -> k n g", g=GS),
+        )
+        fold = const.tile([P, HS], F32)
+        nc.vector.tensor_tensor(out=fold[:], in0=ident[:, 0:HS], in1=ident[:, HS:P], op=ADD)
+        nc.vector.tensor_scalar_mul(out=fold[:], in0=fold[:], scalar1=1.0 / TG)
+        own_half = const.tile([P, H // 2, 2, G], F32)
+        nc.vector.memset(own_half[:], 1.0)
+        nc.vector.memset(own_half[0:HS, :, 1, :], 0.0)
+        nc.vector.memset(own_half[HS:P, :, 0, :], 0.0)
+
+        w_codes = const.tile([P, 3 * C], U32, align_bytes=64)
+        w_scales = const.tile([P, 3 * C], U8, align_bytes=64)
+        x_codes = const.tile([P, NSPAN * C], U32, align_bytes=64)
+        x_scales = const.tile([P, NSPAN * C], U8, align_bytes=64)
+        w_words = w_rows[:].bitcast(F32)
+
+        def prepare(words, matrix, columns, codes, scales, in_head, copy):
+            grouped = stage.tile([P, SETS * P * PACK], BF16, align_bytes=64, name="grouped")
+            grouped_words = grouped[:].bitcast(F32).rearrange("q (s m u) -> q s m u", s=SETS, u=PLANES)
+            current = {}
+
+            def transpose_set(s):
+                if s % 2 == 0:
+                    if in_head:
+                        planes = ps_pass.tile([P, 2, PLANES, P], F32, name="planes", tag="bank")
+                    else:
+                        planes = ps_words.tile([P, 2, PLANES, P], F32, name="planes", tag="words")
+                    current["planes"] = planes
+                planes = current["planes"]
+                for u in range(PLANES):
+                    nc.tensor.transpose(out=planes[:, s % 2, u, :], in_=words(s, u), identity=matrix[:])
+                if s % 2 == 1:
+                    copy(out=grouped_words[:, s - 1 : s + 1], in_=planes[:].rearrange("q s u m -> q s m u"))
+
+            def quantise():
+                nc.vector.quantize_mx(out=codes[:, columns].bitcast(FP8X4), scales=scales[:, columns], in_=grouped[:])
+
+            return [lambda s=s: transpose_set(s) for s in range(SETS)], quantise
+
+        def prepare_w(t, in_head=False):
+            return prepare(
+                lambda s, u: w_words[:, SETS * t + s, u::PLANES],
+                ident,
+                slice(t * C, (t + 1) * C),
+                w_codes,
+                w_scales,
+                in_head,
+                nc.scalar.copy,
+            )
+
+        def prepare_x(span, in_head=False):
+            x_words = x_rows[span][:].bitcast(F32)
+            return prepare(
+                lambda s, u: x_words[:, s * WORDS + u : (s + 1) * WORDS : PLANES],
+                spread,
+                slice(span * C, (span + 1) * C),
+                x_codes,
+                x_scales,
+                in_head,
+                nc.vector.tensor_copy if in_head else nc.scalar.copy,
+            )
+
+        def mx_pass(out, span, j, t):
+            positions = slice((span * J + j) * P, (span * J + j + 1) * P)
+            channels = slice(t * C, (t + 1) * C)
+            nc.tensor.matmul_mx(
+                out=out,
+                lhsT=x_codes[:, positions].bitcast(FP8X4),
+                lhsT_scale=x_scales[:, positions],
+                rhs=w_codes[:, channels].bitcast(FP8X4),
+                rhs_scale=w_scales[:, channels],
+                start=True,
+                stop=True,
+            )
+
+        sets_w, quantise_w = prepare_w(Q_, in_head=True)
+        sets_x, quantise_x = prepare_x(0, in_head=True)
+        for call in sets_w + sets_x:
+            call()
+        quantise_w()
+        quantise_x()
+        neg_sin_t = const.tile([P, NQ, J * NI], BF16)
+        nc.vector.tensor_scalar_mul(out=neg_sin_t[:], in0=sin_t[:], scalar1=-1.0)
+
+        chunks = {}
+        products_of = {}
+        group_sums = {}
+        v_sums = {}
+        waiting = {"reduces": []}
+
+        def store_chunk(span, t):
+            b, qt = divmod(span, NQ)
+            queue = nc.scalar if t == V_ else nc.sync
+            for g in range(GS):
+                queue.dma_start(
+                    out=outs[t][b, :, qt * GS + g, 0:TG, :].rearrange("h (n j) c -> n h (j c)", j=J),
+                    in_=chunks[(span, t)][g:P:GS, :, :, :].rearrange("n h j c -> n h (j c)"),
+                )
+
+        def rope_products(span, t, j):
+            qt = span % NQ
+            if (span, j // 2) not in products_of:
+                cos_prod = products.tile([P, 2 * H, 2, HS], F32, name="cos_prod")
+                sin_prod = products.tile([P, 2, 2 * H, 2, NI], F32, name="sin_prod")
+                products_of[(span, j // 2)] = (cos_prod, sin_prod)
+            cos_prod, sin_prod = products_of[(span, j // 2)]
+            heads = slice(t * H, (t + 1) * H)
+            angles = slice(j * NI, (j + 1) * NI)
+            bank = ps_pass.tile([P, C], F32, name="bank", tag="bank")
+            mx_pass(bank[:], span, j, t)
+            ab = bank[:].rearrange("p (h i x) -> p h i x", h=H, x=2)
+            nc.vector.tensor_tensor(
+                out=cos_prod[:, heads, j % 2, :].rearrange("p h (i x) -> p h i x", x=2),
+                in0=ab,
+                in1=cos_t[:, qt, angles].unsqueeze(1).unsqueeze(3).to_broadcast([P, H, NI, 2]),
+                op=MULT,
+            )
+            nc.vector.tensor_tensor(
+                out=sin_prod[:, 0, heads, j % 2, :],
+                in0=ab[:, :, :, 1],
+                in1=neg_sin_t[:, qt, angles].unsqueeze(1).to_broadcast([P, H, NI]),
+                op=MULT,
+            )
+            nc.vector.tensor_tensor(
+                out=sin_prod[:, 1, heads, j % 2, :],
+                in0=ab[:, :, :, 0],
+                in1=sin_t[:, qt, angles].unsqueeze(1).to_broadcast([P, H, NI]),
+                op=MULT,
+            )
+
+        def rope_add(span, t, slot_pair):
+            if slot_pair == 0:
+                chunk = chunk_pool.tile([P, H, J, HS], F32, name="chunk")
+                chunks[(span, t)] = chunk
+            cos_prod, sin_prod = products_of[(span, slot_pair)]
+            heads = slice(t * H, (t + 1) * H)
+            engine = nc.vector if (span, t) == (NSPAN - 1, K_) else nc.gpsimd
+            engine.tensor_tensor(
+                out=chunks[(span, t)][:, :, 2 * slot_pair : 2 * slot_pair + 2, :].rearrange("p h j (i x) -> p h (j i) x", x=2),
+                in0=cos_prod[:, heads, :, :].rearrange("p h j (i x) -> p h (j i) x", x=2),
+                in1=sin_prod[:, :, heads, :, :].rearrange("p x h j i -> p h (j i) x"),
+                op=ADD,
+            )
+            if slot_pair == 1:
+                store_chunk(span, t)
+
+        def v_slot(span, j):
+            b, qt = divmod(span, NQ)
+            if j == 0:
+                chunk = chunk_pool.tile([P, H, J, HS], F32, name="chunk")
+                chunks[(span, V_)] = chunk
+            bank = ps_pass.tile([P, C], F32, name="bank", tag="bank")
+            mx_pass(bank[:], span, j, V_)
+            nc.scalar.copy(out=chunks[(span, V_)][:, :, j, :], in_=bank[:].rearrange("p (h c) -> p h c", h=H))
+            if j == J - 1:
+                store_chunk(span, V_)
+            v_turned = ps_vt.tile([P, C], F32, name="v_turned")
+            two_heads = slice(V_ * C + j * P, V_ * C + (j + 1) * P)
+            positions = slice(span * C, (span + 1) * C)
+            nc.tensor.matmul_mx(
+                out=v_turned[:],
+                lhsT=w_codes[:, two_heads].bitcast(FP8X4),
+                lhsT_scale=w_scales[:, two_heads],
+                rhs=x_codes[:, positions].bitcast(FP8X4),
+                rhs_scale=x_scales[:, positions],
+                start=True,
+                stop=True,
+            )
+            by_group = v_turned[:].rearrange("m (j n g) -> m g j n", j=J, g=GS)
+            for g in range(GS):
+                unused = small.tile([P, J, P // GS], F32, name="unused")
+                nc.scalar.activation(
+                    out=unused[:],
+                    in_=by_group[:, g],
+                    func=COPY,
+                    accum_out=v_sums[b][:, j, qt * GS + g : qt * GS + g + 1],
+                )
+
+        def sum_tile(n):
+            span, t, first_head = n // SUM_TILES, (n % SUM_TILES) // 2, (n % 2) * HEADS_OF_TILE
+            b, qt = divmod(span, NQ)
+            turned = ps_sums.tile([P, HEADS_OF_TILE, P], F32, name="turned")
+            for h in range(HEADS_OF_TILE):
+                for slot_pair in range(2):
+                    nc.tensor.matmul(
+                        out=turned[:, h, :],
+                        lhsT=chunks[(span, t)][:, first_head + h, 2 * slot_pair : 2 * slot_pair + 2, :].rearrange("p j c -> p (j c)"),
+                        rhs=ident[:],
+                        is_transpose=True,
+                        start=(slot_pair == 0),
+                        stop=(slot_pair == 1),
+                    )
+            waiting["reduces"].append(
+                lambda: nc.vector.tensor_reduce(
+                    out=group_sums[b][:, t, first_head : first_head + HEADS_OF_TILE, qt * GS : (qt + 1) * GS],
+                    in_=turned[:].rearrange("m h (n g) -> m h g n", g=GS),
+                    axis=LAST_AXIS,
+                    op=ADD,
+                )
+            )
+
+        def do_reduces():
+            for call in waiting["reduces"]:
+                call()
+            waiting["reduces"] = []
+
+        def store_means(b):
+            do_reduces()
+            nc.vector.tensor_tensor(
+                out=group_sums[b][:, V_, :, :].rearrange("m (a x) g -> m a x g", x=2),
+                in0=v_sums[b][:].unsqueeze(2).to_broadcast([P, H // 2, 2, G]),
+                in1=own_half[:],
+                op=MULT,
+            )
+            means_ps = ps_words.tile([P, 3 * HS], F32, name="means_ps", tag="words")
+            for t in range(3):
+                nc.tensor.matmul(
+                    out=means_ps[:, t * HS : (t + 1) * HS],
+                    lhsT=group_sums[b][:, t, :, :].rearrange("m h g -> m (h g)"),
+                    rhs=fold[:],
+                    start=True,
+                    stop=True,
+                )
+            means = small.tile([P, 3 * HS], F32, name="means")
+            nc.scalar.copy(out=means[:], in_=means_ps[:])
+            for t in range(3):
+                nc.sync.dma_start(
+                    out=outs[t][b, :, :, TG, :].rearrange("h g c -> (h g) c"),
+                    in_=means[:, t * HS : (t + 1) * HS],
+                )
+
+        first_w = {}
+        next_x = {}
+        for beat in range(NSPAN * BEATS + SUM_LAG):
+            span, s = divmod(beat, BEATS)
+            side = []
+            if span < NSPAN:
+                if s == 0 and span % NQ == 0:
+                    sums_qkv = small.tile([P, 3, H, G], F32, name="sums_qkv")
+                    sums_v = small.tile([P, H // 2, G], F32, name="sums_v")
+                    group_sums[span // NQ] = sums_qkv
+                    v_sums[span // NQ] = sums_v
+                tensor_by_tensor = span == 0 or span == NSPAN - 1
+                if tensor_by_tensor:
+                    passes = [(s // 2, 2 * (s % 2)), (s // 2, 2 * (s % 2) + 1)]
+                    due = [(s // 2, s % 2)]
+                else:
+                    passes = [(Q_, s), (K_, s)]
+                    due = [(Q_, s // 2), (K_, s // 2)] if s % 2 == 1 else []
+                if beat == 0:
+                    first_w[K_] = prepare_w(K_)
+                    first_w[V_] = prepare_w(V_)
+                if s == 0 and span + 1 < NSPAN:
+                    next_x["sets"], next_x["quantise"] = prepare_x(span + 1)
+                if span == 0:
+                    if s == 0:
+                        side += first_w[K_][0]
+                    elif s == 1:
+                        side += [first_w[K_][1]] + first_w[V_][0]
+                    elif s == 2:
+                        side += [first_w[V_][1]] + next_x["sets"] + [lambda: v_slot(0, 0), lambda: v_slot(0, 1)]
+                    else:
+                        side += [next_x["quantise"], lambda: v_slot(0, 2), lambda: v_slot(0, 3)]
+                else:
+                    side.append(lambda: v_slot(span, s))
+                    if span + 1 < NSPAN:
+                        if s < 2:
+                            side += next_x["sets"][2 * s : 2 * s + 2]
+                        elif s == 2:
+                            side.append(next_x["quantise"])
+            n = beat - SUM_LAG
+            if n >= 0:
+                side.append(lambda: sum_tile(n))
+                if n % (NQ * SUM_TILES) == NQ * SUM_TILES - 1:
+                    side.append(lambda: store_means(n // (NQ * SUM_TILES)))
+
+            if span < NSPAN:
+                for t, j in passes:
+                    rope_products(span, t, j)
+            do_reduces()
+            if span < NSPAN:
+                for t, slot_pair in due:
+                    rope_add(span, t, slot_pair)
+            for call in side:
+                call()

@@ -10,7 +10,6 @@ U8 = mybir.dt.uint8
 FP8X4 = mybir.dt.float8_e4m3fn_x4
 ADD = mybir.AluOpType.add
 MULT = mybir.AluOpType.mult
-COPY = mybir.ActivationFunctionType.Copy
 LAST_AXIS = mybir.AxisListType.X
 
 P = 128
@@ -18,18 +17,20 @@ B, T, C, H, G = 2, 2048, 512, 8, 16
 HS = C // H
 NI = HS // 2
 TG = T // G
-J = 4
+J = 8
 GS = P * J // TG
 NQ = T // (P * J)
 NSPAN = B * NQ
+PAIRS = J // 2
 WORDS = C // 2
 PLANES = WORDS // P
 PACK = 4
 SETS = 4
+PARTS = J // SETS
 HEADS_OF_TILE = 4
+HEADS_OF_STEP = 2
 Q_, K_, V_ = 0, 1, 2
-BEATS = 4
-SUM_TILES = 4
+BEATS = 2 * PAIRS
 SUM_LAG = 5
 FLOPS = 2 * B * T * 3 * C * C
 
@@ -41,12 +42,13 @@ def tile_causalselfattention2_pa_t_kernel(tc, x, w_attn, freqs_cos, freqs_sin, o
         const = ctx.enter_context(tc.tile_pool(name="const", bufs=1))
         x_pool = ctx.enter_context(tc.tile_pool(name="x_pool", bufs=NSPAN))
         stage = ctx.enter_context(tc.tile_pool(name="stage", bufs=2))
-        products = ctx.enter_context(tc.tile_pool(name="products", bufs=4))
-        chunk_pool = ctx.enter_context(tc.tile_pool(name="chunk_pool", bufs=7))
+        products = ctx.enter_context(tc.tile_pool(name="products", bufs=6))
+        chunk_pool = ctx.enter_context(tc.tile_pool(name="chunk_pool", bufs=5))
         small = ctx.enter_context(tc.tile_pool(name="small", bufs=2))
         ps_words = ctx.enter_context(tc.psum_pool(name="ps_words", bufs=1))
-        ps_pass = ctx.enter_context(tc.psum_pool(name="ps_pass", bufs=4))
-        ps_vt = ctx.enter_context(tc.psum_pool(name="ps_vt", bufs=1))
+        ps_pass = ctx.enter_context(tc.psum_pool(name="ps_pass", bufs=3))
+        ps_v = ctx.enter_context(tc.psum_pool(name="ps_v", bufs=1))
+        ps_vsum = ctx.enter_context(tc.psum_pool(name="ps_vsum", bufs=1))
         ps_sums = ctx.enter_context(tc.psum_pool(name="ps_sums", bufs=2))
         ctx.enter_context(tc.manual_schedule())
 
@@ -57,30 +59,37 @@ def tile_causalselfattention2_pa_t_kernel(tc, x, w_attn, freqs_cos, freqs_sin, o
             x_span = x_pool.tile([P, J * C], BF16, name="x_span")
             x_rows.append(x_span)
 
-        def load_w(t):
-            nc.sync.dma_start(out=w_rows[:, SETS * t : SETS * (t + 1), :], in_=w_view[:, SETS * t : SETS * (t + 1), :])
+        def load_w(first, sets):
+            nc.sync.dma_start(out=w_rows[:, first : first + sets, :], in_=w_view[:, first : first + sets, :])
 
-        def load_x(span):
+        def load_x(span, first, slots):
             b, qt = divmod(span, NQ)
-            nc.sync.dma_start(
-                out=x_rows[span][:],
-                in_=x[b, qt * P * J : (qt + 1) * P * J, :].rearrange("(p j) k -> p (j k)", j=J),
-            )
+            view = x[b, qt * P * J : (qt + 1) * P * J, :].rearrange("(p j) k -> p (j k)", j=J)
+            columns = slice(first * C, (first + slots) * C)
+            nc.sync.dma_start(out=x_rows[span][:, columns], in_=view[:, columns])
 
-        load_w(Q_)
-        load_x(0)
-        load_w(K_)
-        load_w(V_)
-        for span in range(1, NSPAN):
-            load_x(span)
+        load_w(0, 2)
+        load_x(0, 0, 2)
+        load_w(2, 2)
+        load_x(0, 2, 2)
 
         cos_t = const.tile([P, NQ, J * NI], BF16)
         sin_t = const.tile([P, NQ, J * NI], BF16)
         cos_view = freqs_cos.rearrange("(q g n j) i -> g n q (j i)", q=NQ, g=GS, j=J)
         sin_view = freqs_sin.rearrange("(q g n j) i -> g n q (j i)", q=NQ, g=GS, j=J)
         for g in range(GS):
-            nc.scalar.dma_start(out=cos_t[g:P:GS, :, :], in_=cos_view[g])
-            nc.scalar.dma_start(out=sin_t[g:P:GS, :, :], in_=sin_view[g])
+            nc.sync.dma_start(out=sin_t[g:P:GS, :, :], in_=sin_view[g])
+        for g in range(GS):
+            nc.sync.dma_start(out=cos_t[g:P:GS, :, :], in_=cos_view[g])
+        load_x(0, SETS, SETS)
+        load_w(K_ * SETS, SETS)
+        load_w(V_ * SETS, SETS)
+        for span in range(1, NSPAN):
+            load_x(span, 0, J)
+        table_in = const.tile([P, 1], F32)
+        table_out = const.tile([P, 1], F32)
+        nc.vector.memset(table_in[:], 0.0)
+        nc.scalar.copy(out=table_out[:], in_=table_in[:])
 
         ident = const.tile([P, P], F32)
         make_identity(nc, ident[:])
@@ -96,35 +105,42 @@ def tile_causalselfattention2_pa_t_kernel(tc, x, w_attn, freqs_cos, freqs_sin, o
         nc.vector.memset(own_half[:], 1.0)
         nc.vector.memset(own_half[0:HS, :, 1, :], 0.0)
         nc.vector.memset(own_half[HS:P, :, 0, :], 0.0)
+        sign = const.tile([P, 2], F32)
+        nc.gpsimd.memset(sign[:, 0:1], -1.0)
+        nc.gpsimd.memset(sign[:, 1:2], 1.0)
+        turn_t = const.tile([P, NQ, J * NI, 2], BF16)
+        for q in range(NQ):
+            nc.gpsimd.tensor_tensor(
+                out=turn_t[:, q],
+                in0=sin_t[:, q].unsqueeze(2).to_broadcast([P, J * NI, 2]),
+                in1=sign[:].unsqueeze(1).to_broadcast([P, J * NI, 2]),
+                op=MULT,
+            )
 
         w_codes = const.tile([P, 3 * C], U32, align_bytes=64)
         w_scales = const.tile([P, 3 * C], U8, align_bytes=64)
-        x_codes = const.tile([P, NSPAN * C], U32, align_bytes=64)
-        x_scales = const.tile([P, NSPAN * C], U8, align_bytes=64)
+        x_codes = const.tile([P, NSPAN * J * P], U32, align_bytes=64)
+        x_scales = const.tile([P, NSPAN * J * P], U8, align_bytes=64)
         w_words = w_rows[:].bitcast(F32)
 
         def prepare(words, matrix, columns, codes, scales, in_head, copy):
             grouped = stage.tile([P, SETS * P * PACK], BF16, align_bytes=64, name="grouped")
             grouped_words = grouped[:].bitcast(F32).rearrange("q (s m u) -> q s m u", s=SETS, u=PLANES)
-            current = {}
 
-            def transpose_set(s):
-                if s % 2 == 0:
-                    if in_head:
-                        planes = ps_pass.tile([P, 2, PLANES, P], F32, name="planes", tag="bank")
-                    else:
-                        planes = ps_words.tile([P, 2, PLANES, P], F32, name="planes", tag="words")
-                    current["planes"] = planes
-                planes = current["planes"]
-                for u in range(PLANES):
-                    nc.tensor.transpose(out=planes[:, s % 2, u, :], in_=words(s, u), identity=matrix[:])
-                if s % 2 == 1:
-                    copy(out=grouped_words[:, s - 1 : s + 1], in_=planes[:].rearrange("q s u m -> q s m u"))
+            def transpose_two(s):
+                if in_head:
+                    planes = ps_pass.tile([P, 2, PLANES, P], F32, name="planes", tag="bank")
+                else:
+                    planes = ps_words.tile([P, 2, PLANES, P], F32, name="planes", tag="words")
+                for i in range(2):
+                    for u in range(PLANES):
+                        nc.tensor.transpose(out=planes[:, i, u, :], in_=words(s + i, u), identity=matrix[:])
+                copy(out=grouped_words[:, s : s + 2], in_=planes[:].rearrange("q s u m -> q s m u"))
 
             def quantise():
                 nc.vector.quantize_mx(out=codes[:, columns].bitcast(FP8X4), scales=scales[:, columns], in_=grouped[:])
 
-            return [lambda s=s: transpose_set(s) for s in range(SETS)], quantise
+            return [lambda s=s: transpose_two(s) for s in range(0, SETS, 2)], quantise
 
         def prepare_w(t, in_head=False):
             return prepare(
@@ -137,12 +153,13 @@ def tile_causalselfattention2_pa_t_kernel(tc, x, w_attn, freqs_cos, freqs_sin, o
                 nc.scalar.copy,
             )
 
-        def prepare_x(span, in_head=False):
+        def prepare_x(span, part, in_head=False):
             x_words = x_rows[span][:].bitcast(F32)
+            first = (span * J + part * SETS) * P
             return prepare(
-                lambda s, u: x_words[:, s * WORDS + u : (s + 1) * WORDS : PLANES],
+                lambda s, u: x_words[:, (part * SETS + s) * WORDS + u : (part * SETS + s + 1) * WORDS : PLANES],
                 spread,
-                slice(span * C, (span + 1) * C),
+                slice(first, first + SETS * P),
                 x_codes,
                 x_scales,
                 in_head,
@@ -163,130 +180,132 @@ def tile_causalselfattention2_pa_t_kernel(tc, x, w_attn, freqs_cos, freqs_sin, o
             )
 
         sets_w, quantise_w = prepare_w(Q_, in_head=True)
-        sets_x, quantise_x = prepare_x(0, in_head=True)
-        for call in sets_w + sets_x:
-            call()
+        sets_x, quantise_x = prepare_x(0, 0, in_head=True)
+        for call_w, call_x in zip(sets_w, sets_x):
+            call_w()
+            call_x()
         quantise_w()
         quantise_x()
-        neg_sin_t = const.tile([P, NQ, J * NI], BF16)
-        nc.vector.tensor_scalar_mul(out=neg_sin_t[:], in0=sin_t[:], scalar1=-1.0)
 
         chunks = {}
         products_of = {}
+        banks = {}
         group_sums = {}
         v_sums = {}
         waiting = {"reduces": []}
 
-        def store_chunk(span, t):
+        def store_chunk(span, t, first=0, slots=J):
             b, qt = divmod(span, NQ)
-            queue = nc.scalar if t == V_ else nc.sync
-            for g in range(GS):
-                queue.dma_start(
-                    out=outs[t][b, :, qt * GS + g, 0:TG, :].rearrange("h (n j) c -> n h (j c)", j=J),
-                    in_=chunks[(span, t)][g:P:GS, :, :, :].rearrange("n h j c -> n h (j c)"),
+            for i in range(GS):
+                g = (i // 2) + (i % 2) * (GS // 2)
+                nc.sync.dma_start(
+                    out=outs[t][b, :, qt * GS + g, 0:TG, :].rearrange("h (n j) c -> n h (j c)", j=J)[:, :, first * HS : (first + slots) * HS],
+                    in_=chunks[(span, t)][g:P:GS, :, first : first + slots, :].rearrange("n h j c -> n h (j c)"),
                 )
+
+        def new_chunk(span, t):
+            chunk = chunk_pool.tile([P, H, J, HS], F32, name="chunk")
+            chunks[(span, t)] = chunk
+
+        def rope_pass(m):
+            if m < NSPAN * 2 * J:
+                bank = ps_pass.tile([P, C], F32, name="bank", tag="bank")
+                mx_pass(bank[:], m // (2 * J), m % J, m // J % 2)
+                banks[m] = bank
 
         def rope_products(span, t, j):
             qt = span % NQ
-            if (span, j // 2) not in products_of:
-                cos_prod = products.tile([P, 2 * H, 2, HS], F32, name="cos_prod")
-                sin_prod = products.tile([P, 2, 2 * H, 2, NI], F32, name="sin_prod")
-                products_of[(span, j // 2)] = (cos_prod, sin_prod)
-            cos_prod, sin_prod = products_of[(span, j // 2)]
-            heads = slice(t * H, (t + 1) * H)
+            if j % 2 == 0:
+                cos_prod = products.tile([P, H, 2, HS], F32, name="cos_prod")
+                sin_prod = products.tile([P, H, 2, HS], F32, name="sin_prod")
+                products_of[(span, t)] = (cos_prod, sin_prod)
+            cos_prod, sin_prod = products_of[(span, t)]
             angles = slice(j * NI, (j + 1) * NI)
-            bank = ps_pass.tile([P, C], F32, name="bank", tag="bank")
-            mx_pass(bank[:], span, j, t)
-            ab = bank[:].rearrange("p (h i x) -> p h i x", h=H, x=2)
+            ab = banks[(span * 2 + t) * J + j][:].rearrange("p (h i x) -> p h i x", h=H, x=2)
             nc.vector.tensor_tensor(
-                out=cos_prod[:, heads, j % 2, :].rearrange("p h (i x) -> p h i x", x=2),
+                out=cos_prod[:, :, j % 2, :].rearrange("p h (i x) -> p h i x", x=2),
                 in0=ab,
                 in1=cos_t[:, qt, angles].unsqueeze(1).unsqueeze(3).to_broadcast([P, H, NI, 2]),
                 op=MULT,
             )
             nc.vector.tensor_tensor(
-                out=sin_prod[:, 0, heads, j % 2, :],
-                in0=ab[:, :, :, 1],
-                in1=neg_sin_t[:, qt, angles].unsqueeze(1).to_broadcast([P, H, NI]),
-                op=MULT,
-            )
-            nc.vector.tensor_tensor(
-                out=sin_prod[:, 1, heads, j % 2, :],
-                in0=ab[:, :, :, 0],
-                in1=sin_t[:, qt, angles].unsqueeze(1).to_broadcast([P, H, NI]),
+                out=sin_prod[:, :, j % 2, :].rearrange("p h (i x) -> p h i x", x=2),
+                in0=ab[:, :, :, ::-1],
+                in1=turn_t[:, qt, angles].unsqueeze(1).to_broadcast([P, H, NI, 2]),
                 op=MULT,
             )
 
-        def rope_add(span, t, slot_pair):
-            if slot_pair == 0:
-                chunk = chunk_pool.tile([P, H, J, HS], F32, name="chunk")
-                chunks[(span, t)] = chunk
-            cos_prod, sin_prod = products_of[(span, slot_pair)]
-            heads = slice(t * H, (t + 1) * H)
-            engine = nc.vector if (span, t) == (NSPAN - 1, K_) else nc.gpsimd
+        def rope_add(span, t, pair):
+            if pair == 0:
+                new_chunk(span, t)
+            cos_prod, sin_prod = products_of[(span, t)]
+            engine = nc.vector if (span, t, pair) == (NSPAN - 1, K_, PAIRS - 1) else nc.gpsimd
             engine.tensor_tensor(
-                out=chunks[(span, t)][:, :, 2 * slot_pair : 2 * slot_pair + 2, :].rearrange("p h j (i x) -> p h (j i) x", x=2),
-                in0=cos_prod[:, heads, :, :].rearrange("p h j (i x) -> p h (j i) x", x=2),
-                in1=sin_prod[:, :, heads, :, :].rearrange("p x h j i -> p h (j i) x"),
-                op=ADD,
+                out=chunks[(span, t)][:, :, 2 * pair : 2 * pair + 2, :], in0=cos_prod[:], in1=sin_prod[:], op=ADD
             )
-            if slot_pair == 1:
-                store_chunk(span, t)
 
         def v_slot(span, j):
-            b, qt = divmod(span, NQ)
             if j == 0:
-                chunk = chunk_pool.tile([P, H, J, HS], F32, name="chunk")
-                chunks[(span, V_)] = chunk
-            bank = ps_pass.tile([P, C], F32, name="bank", tag="bank")
+                new_chunk(span, V_)
+            bank = ps_v.tile([P, C], F32, name="v_bank")
             mx_pass(bank[:], span, j, V_)
             nc.scalar.copy(out=chunks[(span, V_)][:, :, j, :], in_=bank[:].rearrange("p (h c) -> p h c", h=H))
             if j == J - 1:
                 store_chunk(span, V_)
-            v_turned = ps_vt.tile([P, C], F32, name="v_turned")
-            two_heads = slice(V_ * C + j * P, V_ * C + (j + 1) * P)
-            positions = slice(span * C, (span + 1) * C)
-            nc.tensor.matmul_mx(
-                out=v_turned[:],
-                lhsT=w_codes[:, two_heads].bitcast(FP8X4),
-                lhsT_scale=w_scales[:, two_heads],
-                rhs=x_codes[:, positions].bitcast(FP8X4),
-                rhs_scale=x_scales[:, positions],
-                start=True,
-                stop=True,
-            )
-            by_group = v_turned[:].rearrange("m (j n g) -> m g j n", j=J, g=GS)
-            for g in range(GS):
-                unused = small.tile([P, J, P // GS], F32, name="unused")
-                nc.scalar.activation(
-                    out=unused[:],
-                    in_=by_group[:, g],
-                    func=COPY,
-                    accum_out=v_sums[b][:, j, qt * GS + g : qt * GS + g + 1],
-                )
 
-        def sum_tile(n):
-            span, t, first_head = n // SUM_TILES, (n % SUM_TILES) // 2, (n % 2) * HEADS_OF_TILE
+        def v_sum(span, two):
             b, qt = divmod(span, NQ)
-            turned = ps_sums.tile([P, HEADS_OF_TILE, P], F32, name="turned")
-            for h in range(HEADS_OF_TILE):
-                for slot_pair in range(2):
-                    nc.tensor.matmul(
-                        out=turned[:, h, :],
-                        lhsT=chunks[(span, t)][:, first_head + h, 2 * slot_pair : 2 * slot_pair + 2, :].rearrange("p j c -> p (j c)"),
-                        rhs=ident[:],
-                        is_transpose=True,
-                        start=(slot_pair == 0),
-                        stop=(slot_pair == 1),
-                    )
+            v_turned = ps_vsum.tile([P, P], F32, name="v_turned")
+            channels = slice(V_ * C + two * P, V_ * C + (two + 1) * P)
+            for j in range(J):
+                positions = slice((span * J + j) * P, (span * J + j + 1) * P)
+                nc.tensor.matmul_mx(
+                    out=v_turned[:],
+                    lhsT=w_codes[:, channels].bitcast(FP8X4),
+                    lhsT_scale=w_scales[:, channels],
+                    rhs=x_codes[:, positions].bitcast(FP8X4),
+                    rhs_scale=x_scales[:, positions],
+                    start=(j == 0),
+                    stop=(j == J - 1),
+                )
             waiting["reduces"].append(
                 lambda: nc.vector.tensor_reduce(
-                    out=group_sums[b][:, t, first_head : first_head + HEADS_OF_TILE, qt * GS : (qt + 1) * GS],
-                    in_=turned[:].rearrange("m h (n g) -> m h g n", g=GS),
+                    out=v_sums[b][:, two, qt * GS : (qt + 1) * GS],
+                    in_=v_turned[:].rearrange("m (n g) -> m g n", g=GS),
                     axis=LAST_AXIS,
                     op=ADD,
                 )
             )
+
+        def sum_step(n):
+            chunk_index, step = divmod(n, H // HEADS_OF_STEP)
+            span, t = divmod(chunk_index, 2)
+            b, qt = divmod(span, NQ)
+            if step % 2 == 0:
+                turned = ps_sums.tile([P, HEADS_OF_TILE, P], F32, name="turned")
+                waiting["turned"] = turned
+            turned = waiting["turned"]
+            for i in range(HEADS_OF_STEP):
+                h = step * HEADS_OF_STEP + i
+                for pair in range(PAIRS):
+                    nc.tensor.matmul(
+                        out=turned[:, h % HEADS_OF_TILE, :],
+                        lhsT=chunks[(span, t)][:, h, 2 * pair : 2 * pair + 2, :].rearrange("p j c -> p (j c)"),
+                        rhs=ident[:],
+                        is_transpose=True,
+                        start=(pair == 0),
+                        stop=(pair == PAIRS - 1),
+                    )
+            if step % 2 == 1:
+                first_head = (step // 2) * HEADS_OF_TILE
+                waiting["reduces"].append(
+                    lambda: nc.vector.tensor_reduce(
+                        out=group_sums[b][:, t, first_head : first_head + HEADS_OF_TILE, qt * GS : (qt + 1) * GS],
+                        in_=turned[:].rearrange("m h (n g) -> m h g n", g=GS),
+                        axis=LAST_AXIS,
+                        op=ADD,
+                    )
+                )
 
         def do_reduces():
             for call in waiting["reduces"]:
@@ -318,57 +337,65 @@ def tile_causalselfattention2_pa_t_kernel(tc, x, w_attn, freqs_cos, freqs_sin, o
                     in_=means[:, t * HS : (t + 1) * HS],
                 )
 
-        first_w = {}
-        next_x = {}
+        rope_pass(0)
+        sums_per_sequence = NQ * 2 * (H // HEADS_OF_STEP)
+        prepared = {"quantise": None, "sets": []}
         for beat in range(NSPAN * BEATS + SUM_LAG):
             span, s = divmod(beat, BEATS)
             side = []
             if span < NSPAN:
+                t, pair = divmod(s, PAIRS)
                 if s == 0 and span % NQ == 0:
                     sums_qkv = small.tile([P, 3, H, G], F32, name="sums_qkv")
                     sums_v = small.tile([P, H // 2, G], F32, name="sums_v")
                     group_sums[span // NQ] = sums_qkv
                     v_sums[span // NQ] = sums_v
-                tensor_by_tensor = span == 0 or span == NSPAN - 1
-                if tensor_by_tensor:
-                    passes = [(s // 2, 2 * (s % 2)), (s // 2, 2 * (s % 2) + 1)]
-                    due = [(s // 2, s % 2)]
-                else:
-                    passes = [(Q_, s), (K_, s)]
-                    due = [(Q_, s // 2), (K_, s // 2)] if s % 2 == 1 else []
-                if beat == 0:
-                    first_w[K_] = prepare_w(K_)
-                    first_w[V_] = prepare_w(V_)
-                if s == 0 and span + 1 < NSPAN:
-                    next_x["sets"], next_x["quantise"] = prepare_x(span + 1)
+                quantise_now = prepared["quantise"]
+                prepared["quantise"] = None
+                two_sets = []
                 if span == 0:
-                    if s == 0:
-                        side += first_w[K_][0]
-                    elif s == 1:
-                        side += [first_w[K_][1]] + first_w[V_][0]
-                    elif s == 2:
-                        side += [first_w[V_][1]] + next_x["sets"] + [lambda: v_slot(0, 0), lambda: v_slot(0, 1)]
-                    else:
-                        side += [next_x["quantise"], lambda: v_slot(0, 2), lambda: v_slot(0, 3)]
+                    operand = [("x", 0, 1), ("w", K_), ("w", V_), None, ("x", 1, 0), None, ("x", 1, 1), None][s]
+                    whole = s < 2
+                    v_now = [2 * (s - 4), 2 * (s - 4) + 1] if s >= 4 else []
+                    v_sums_now = [s - 4] if s >= 4 else []
                 else:
-                    side.append(lambda: v_slot(span, s))
-                    if span + 1 < NSPAN:
-                        if s < 2:
-                            side += next_x["sets"][2 * s : 2 * s + 2]
-                        elif s == 2:
-                            side.append(next_x["quantise"])
+                    operand = ("x", span + 1, s // 4) if span + 1 < NSPAN and s % 4 == 0 else None
+                    whole = False
+                    v_now = [s]
+                    v_sums_now = [s // 2] if s % 2 == 1 else []
+                if operand is not None:
+                    sets, quantise = prepare_x(operand[1], operand[2]) if operand[0] == "x" else prepare_w(operand[1])
+                    prepared["sets"] = sets
+                    prepared["next"] = quantise
+                for i in range(2 if whole else 1):
+                    if prepared["sets"]:
+                        two_sets.append(prepared["sets"][0])
+                        prepared["sets"] = prepared["sets"][1:]
+                        if not prepared["sets"]:
+                            prepared["quantise"] = prepared["next"]
+                for j in v_now[0:1]:
+                    side.append(lambda j=j: v_slot(span, j))
+                side += two_sets
+                for j in v_now[1:]:
+                    side.append(lambda j=j: v_slot(span, j))
+                for two in v_sums_now:
+                    side.append(lambda two=two: v_sum(span, two))
             n = beat - SUM_LAG
             if n >= 0:
-                side.append(lambda: sum_tile(n))
-                if n % (NQ * SUM_TILES) == NQ * SUM_TILES - 1:
-                    side.append(lambda: store_means(n // (NQ * SUM_TILES)))
+                side.append(lambda: sum_step(n))
+                if n % sums_per_sequence == sums_per_sequence - 1:
+                    side.append(lambda: store_means(n // sums_per_sequence))
 
             if span < NSPAN:
-                for t, j in passes:
+                for j in (2 * pair, 2 * pair + 1):
+                    rope_pass((span * 2 + t) * J + j + 1)
                     rope_products(span, t, j)
+                    if j % 2 == 0 and quantise_now is not None:
+                        quantise_now()
             do_reduces()
             if span < NSPAN:
-                for t, slot_pair in due:
-                    rope_add(span, t, slot_pair)
+                rope_add(span, t, pair)
             for call in side:
                 call()
+            if span < NSPAN and pair == PAIRS - 1:
+                store_chunk(span, t)

@@ -17,9 +17,9 @@ B, T, C, H, G = 2, 2048, 512, 8, 16
 HS = C // H
 NI = HS // 2
 TG = T // G
+SLOTS = T // P
 J = 8
-GS = P * J // TG
-NQ = T // (P * J)
+NQ = SLOTS // J
 NSPAN = B * NQ
 PAIRS = J // 2
 WORDS = C // 2
@@ -64,23 +64,20 @@ def tile_causalselfattention2_pa_t_kernel(tc, x, w_attn, freqs_cos, freqs_sin, o
 
         def load_x(span, first, slots):
             b, qt = divmod(span, NQ)
-            view = x[b, qt * P * J : (qt + 1) * P * J, :].rearrange("(p j) k -> p (j k)", j=J)
+            view = x[b].rearrange("(p j) k -> p (j k)", j=SLOTS)
             columns = slice(first * C, (first + slots) * C)
-            nc.sync.dma_start(out=x_rows[span][:, columns], in_=view[:, columns])
+            start = qt * J * C
+            nc.sync.dma_start(out=x_rows[span][:, columns], in_=view[:, start + first * C : start + (first + slots) * C])
 
         load_w(0, 2)
         load_x(0, 0, 2)
         load_w(2, 2)
         load_x(0, 2, 2)
 
-        cos_t = const.tile([P, NQ, J * NI], BF16)
-        sin_t = const.tile([P, NQ, J * NI], BF16)
-        cos_view = freqs_cos.rearrange("(q g n j) i -> g n q (j i)", q=NQ, g=GS, j=J)
-        sin_view = freqs_sin.rearrange("(q g n j) i -> g n q (j i)", q=NQ, g=GS, j=J)
-        for g in range(GS):
-            nc.sync.dma_start(out=sin_t[g:P:GS, :, :], in_=sin_view[g])
-        for g in range(GS):
-            nc.sync.dma_start(out=cos_t[g:P:GS, :, :], in_=cos_view[g])
+        cos_t = const.tile([P, SLOTS * NI], BF16)
+        sin_t = const.tile([P, SLOTS * NI], BF16)
+        nc.sync.dma_start(out=sin_t[:], in_=freqs_sin.rearrange("(p j) i -> p (j i)", j=SLOTS))
+        nc.sync.dma_start(out=cos_t[:], in_=freqs_cos.rearrange("(p j) i -> p (j i)", j=SLOTS))
         load_x(0, SETS, SETS)
         load_w(K_ * SETS, SETS)
         load_w(V_ * SETS, SETS)
@@ -93,11 +90,6 @@ def tile_causalselfattention2_pa_t_kernel(tc, x, w_attn, freqs_cos, freqs_sin, o
 
         ident = const.tile([P, P], F32)
         make_identity(nc, ident[:])
-        spread = const.tile([P, P], F32)
-        nc.vector.tensor_copy(
-            out=spread[:].rearrange("k (n g) -> k n g", g=GS),
-            in_=ident[:].rearrange("k (g n) -> k n g", g=GS),
-        )
         fold = const.tile([P, HS], F32)
         nc.vector.tensor_tensor(out=fold[:], in0=ident[:, 0:HS], in1=ident[:, HS:P], op=ADD)
         nc.vector.tensor_scalar_mul(out=fold[:], in0=fold[:], scalar1=1.0 / TG)
@@ -108,11 +100,12 @@ def tile_causalselfattention2_pa_t_kernel(tc, x, w_attn, freqs_cos, freqs_sin, o
         sign = const.tile([P, 2], F32)
         nc.gpsimd.memset(sign[:, 0:1], -1.0)
         nc.gpsimd.memset(sign[:, 1:2], 1.0)
-        turn_t = const.tile([P, NQ, J * NI, 2], BF16)
+        turn_t = const.tile([P, SLOTS * NI, 2], BF16)
         for q in range(NQ):
+            angles = slice(q * J * NI, (q + 1) * J * NI)
             nc.gpsimd.tensor_tensor(
-                out=turn_t[:, q],
-                in0=sin_t[:, q].unsqueeze(2).to_broadcast([P, J * NI, 2]),
+                out=turn_t[:, angles, :],
+                in0=sin_t[:, angles].unsqueeze(2).to_broadcast([P, J * NI, 2]),
                 in1=sign[:].unsqueeze(1).to_broadcast([P, J * NI, 2]),
                 op=MULT,
             )
@@ -158,7 +151,7 @@ def tile_causalselfattention2_pa_t_kernel(tc, x, w_attn, freqs_cos, freqs_sin, o
             first = (span * J + part * SETS) * P
             return prepare(
                 lambda s, u: x_words[:, (part * SETS + s) * WORDS + u : (part * SETS + s + 1) * WORDS : PLANES],
-                spread,
+                ident,
                 slice(first, first + SETS * P),
                 x_codes,
                 x_scales,
@@ -194,13 +187,12 @@ def tile_causalselfattention2_pa_t_kernel(tc, x, w_attn, freqs_cos, freqs_sin, o
         v_sums = {}
         waiting = {"reduces": []}
 
-        def store_chunk(span, t, first=0, slots=J):
+        def store_chunk(span, t):
             b, qt = divmod(span, NQ)
-            for i in range(GS):
-                g = (i // 2) + (i % 2) * (GS // 2)
+            for h in range(H):
                 nc.sync.dma_start(
-                    out=outs[t][b, :, qt * GS + g, 0:TG, :].rearrange("h (n j) c -> n h (j c)", j=J)[:, :, first * HS : (first + slots) * HS],
-                    in_=chunks[(span, t)][g:P:GS, :, first : first + slots, :].rearrange("n h j c -> n h (j c)"),
+                    out=outs[t][b, h, :, 0:TG, :].rearrange("g (n j) c -> g n (j c)", j=SLOTS)[:, :, qt * J * HS : (qt + 1) * J * HS],
+                    in_=chunks[(span, t)][:, h, :, :].rearrange("p j c -> p (j c)"),
                 )
 
         def new_chunk(span, t):
@@ -220,18 +212,18 @@ def tile_causalselfattention2_pa_t_kernel(tc, x, w_attn, freqs_cos, freqs_sin, o
                 sin_prod = products.tile([P, H, 2, HS], F32, name="sin_prod")
                 products_of[(span, t)] = (cos_prod, sin_prod)
             cos_prod, sin_prod = products_of[(span, t)]
-            angles = slice(j * NI, (j + 1) * NI)
+            angles = slice((qt * J + j) * NI, (qt * J + j + 1) * NI)
             ab = banks[(span * 2 + t) * J + j][:].rearrange("p (h i x) -> p h i x", h=H, x=2)
             nc.vector.tensor_tensor(
                 out=cos_prod[:, :, j % 2, :].rearrange("p h (i x) -> p h i x", x=2),
                 in0=ab,
-                in1=cos_t[:, qt, angles].unsqueeze(1).unsqueeze(3).to_broadcast([P, H, NI, 2]),
+                in1=cos_t[:, angles].unsqueeze(1).unsqueeze(3).to_broadcast([P, H, NI, 2]),
                 op=MULT,
             )
             nc.vector.tensor_tensor(
                 out=sin_prod[:, :, j % 2, :].rearrange("p h (i x) -> p h i x", x=2),
                 in0=ab[:, :, :, ::-1],
-                in1=turn_t[:, qt, angles].unsqueeze(1).to_broadcast([P, H, NI, 2]),
+                in1=turn_t[:, angles, :].unsqueeze(1).to_broadcast([P, H, NI, 2]),
                 op=MULT,
             )
 
@@ -270,8 +262,8 @@ def tile_causalselfattention2_pa_t_kernel(tc, x, w_attn, freqs_cos, freqs_sin, o
                 )
             waiting["reduces"].append(
                 lambda: nc.vector.tensor_reduce(
-                    out=v_sums[b][:, two, qt * GS : (qt + 1) * GS],
-                    in_=v_turned[:].rearrange("m (n g) -> m g n", g=GS),
+                    out=v_sums[b][:, qt, two, :],
+                    in_=v_turned[:].rearrange("m (g n) -> m g n", g=G),
                     axis=LAST_AXIS,
                     op=ADD,
                 )
@@ -300,8 +292,8 @@ def tile_causalselfattention2_pa_t_kernel(tc, x, w_attn, freqs_cos, freqs_sin, o
                 first_head = (step // 2) * HEADS_OF_TILE
                 waiting["reduces"].append(
                     lambda: nc.vector.tensor_reduce(
-                        out=group_sums[b][:, t, first_head : first_head + HEADS_OF_TILE, qt * GS : (qt + 1) * GS],
-                        in_=turned[:].rearrange("m h (n g) -> m h g n", g=GS),
+                        out=group_sums[b][:, qt, t, first_head : first_head + HEADS_OF_TILE, :],
+                        in_=turned[:].rearrange("m h (g n) -> m h g n", g=G),
                         axis=LAST_AXIS,
                         op=ADD,
                     )
@@ -314,21 +306,23 @@ def tile_causalselfattention2_pa_t_kernel(tc, x, w_attn, freqs_cos, freqs_sin, o
 
         def store_means(b):
             do_reduces()
-            nc.vector.tensor_tensor(
-                out=group_sums[b][:, V_, :, :].rearrange("m (a x) g -> m a x g", x=2),
-                in0=v_sums[b][:].unsqueeze(2).to_broadcast([P, H // 2, 2, G]),
-                in1=own_half[:],
-                op=MULT,
-            )
+            for qt in range(NQ):
+                nc.vector.tensor_tensor(
+                    out=group_sums[b][:, qt, V_, :, :].rearrange("m (a x) g -> m a x g", x=2),
+                    in0=v_sums[b][:, qt].unsqueeze(2).to_broadcast([P, H // 2, 2, G]),
+                    in1=own_half[:],
+                    op=MULT,
+                )
             means_ps = ps_words.tile([P, 3 * HS], F32, name="means_ps", tag="words")
             for t in range(3):
-                nc.tensor.matmul(
-                    out=means_ps[:, t * HS : (t + 1) * HS],
-                    lhsT=group_sums[b][:, t, :, :].rearrange("m h g -> m (h g)"),
-                    rhs=fold[:],
-                    start=True,
-                    stop=True,
-                )
+                for qt in range(NQ):
+                    nc.tensor.matmul(
+                        out=means_ps[:, t * HS : (t + 1) * HS],
+                        lhsT=group_sums[b][:, qt, t, :, :].rearrange("m h g -> m (h g)"),
+                        rhs=fold[:],
+                        start=(qt == 0),
+                        stop=(qt == NQ - 1),
+                    )
             means = small.tile([P, 3 * HS], F32, name="means")
             nc.scalar.copy(out=means[:], in_=means_ps[:])
             for t in range(3):
@@ -346,8 +340,8 @@ def tile_causalselfattention2_pa_t_kernel(tc, x, w_attn, freqs_cos, freqs_sin, o
             if span < NSPAN:
                 t, pair = divmod(s, PAIRS)
                 if s == 0 and span % NQ == 0:
-                    sums_qkv = small.tile([P, 3, H, G], F32, name="sums_qkv")
-                    sums_v = small.tile([P, H // 2, G], F32, name="sums_v")
+                    sums_qkv = small.tile([P, NQ, 3, H, G], F32, name="sums_qkv")
+                    sums_v = small.tile([P, NQ, H // 2, G], F32, name="sums_v")
                     group_sums[span // NQ] = sums_qkv
                     v_sums[span // NQ] = sums_v
                 quantise_now = prepared["quantise"]

@@ -42,7 +42,7 @@ def tile_causalselfattention2_pa_t_kernel(tc, x, w_attn, freqs_cos, freqs_sin, o
         const = ctx.enter_context(tc.tile_pool(name="const", bufs=1))
         x_pool = ctx.enter_context(tc.tile_pool(name="x_pool", bufs=NSPAN))
         stage = ctx.enter_context(tc.tile_pool(name="stage", bufs=2))
-        products = ctx.enter_context(tc.tile_pool(name="products", bufs=6))
+        products = ctx.enter_context(tc.tile_pool(name="products", bufs=5))
         chunk_pool = ctx.enter_context(tc.tile_pool(name="chunk_pool", bufs=5))
         small = ctx.enter_context(tc.tile_pool(name="small", bufs=2))
         ps_words = ctx.enter_context(tc.psum_pool(name="ps_words", bufs=1))
@@ -76,8 +76,8 @@ def tile_causalselfattention2_pa_t_kernel(tc, x, w_attn, freqs_cos, freqs_sin, o
 
         cos_t = const.tile([P, SLOTS * NI], BF16)
         sin_t = const.tile([P, SLOTS * NI], BF16)
-        nc.sync.dma_start(out=sin_t[:], in_=freqs_sin.rearrange("(p j) i -> p (j i)", j=SLOTS))
         nc.sync.dma_start(out=cos_t[:], in_=freqs_cos.rearrange("(p j) i -> p (j i)", j=SLOTS))
+        nc.sync.dma_start(out=sin_t[:], in_=freqs_sin.rearrange("(p j) i -> p (j i)", j=SLOTS))
         load_x(0, SETS, SETS)
         load_w(K_ * SETS, SETS)
         load_w(V_ * SETS, SETS)
@@ -97,18 +97,18 @@ def tile_causalselfattention2_pa_t_kernel(tc, x, w_attn, freqs_cos, freqs_sin, o
         nc.vector.memset(own_half[:], 1.0)
         nc.vector.memset(own_half[0:HS, :, 1, :], 0.0)
         nc.vector.memset(own_half[HS:P, :, 0, :], 0.0)
-        sign = const.tile([P, 2], F32)
-        nc.gpsimd.memset(sign[:, 0:1], -1.0)
-        nc.gpsimd.memset(sign[:, 1:2], 1.0)
-        turn_t = const.tile([P, SLOTS * NI, 2], BF16)
-        for q in range(NQ):
-            angles = slice(q * J * NI, (q + 1) * J * NI)
-            nc.gpsimd.tensor_tensor(
-                out=turn_t[:, angles, :],
-                in0=sin_t[:, angles].unsqueeze(2).to_broadcast([P, J * NI, 2]),
-                in1=sign[:].unsqueeze(1).to_broadcast([P, J * NI, 2]),
-                op=MULT,
-            )
+        sign = const.tile([P, 2, 2], F32)
+        nc.gpsimd.memset(sign[:], 1.0)
+        nc.gpsimd.memset(sign[:, 1, 1:2], -1.0)
+        factors = const.tile([P, SLOTS, 2, HS], BF16)
+        for first in (0, J):
+            for which, table in enumerate((cos_t, sin_t)):
+                nc.gpsimd.tensor_tensor(
+                    out=factors[:, first : first + J, which, :].rearrange("p s (i x) -> p s i x", x=2),
+                    in0=table[:, first * NI : (first + J) * NI].rearrange("p (s i) -> p s i", s=J).unsqueeze(3).to_broadcast([P, J, NI, 2]),
+                    in1=sign[:, which, :].unsqueeze(1).unsqueeze(1).to_broadcast([P, J, NI, 2]),
+                    op=MULT,
+                )
 
         w_codes = const.tile([P, 3 * C], U32, align_bytes=64)
         w_scales = const.tile([P, 3 * C], U8, align_bytes=64)
@@ -208,32 +208,26 @@ def tile_causalselfattention2_pa_t_kernel(tc, x, w_attn, freqs_cos, freqs_sin, o
         def rope_products(span, t, j):
             qt = span % NQ
             if j % 2 == 0:
-                cos_prod = products.tile([P, H, 2, HS], F32, name="cos_prod")
-                sin_prod = products.tile([P, H, 2, HS], F32, name="sin_prod")
-                products_of[(span, t)] = (cos_prod, sin_prod)
-            cos_prod, sin_prod = products_of[(span, t)]
-            angles = slice((qt * J + j) * NI, (qt * J + j + 1) * NI)
-            ab = banks[(span * 2 + t) * J + j][:].rearrange("p (h i x) -> p h i x", h=H, x=2)
+                both = products.tile([P, 2, H, 2, HS], F32, name="both")
+                products_of[(span, t)] = both
+            both = products_of[(span, t)]
             nc.vector.tensor_tensor(
-                out=cos_prod[:, :, j % 2, :].rearrange("p h (i x) -> p h i x", x=2),
-                in0=ab,
-                in1=cos_t[:, angles].unsqueeze(1).unsqueeze(3).to_broadcast([P, H, NI, 2]),
-                op=MULT,
-            )
-            nc.vector.tensor_tensor(
-                out=sin_prod[:, :, j % 2, :].rearrange("p h (i x) -> p h i x", x=2),
-                in0=ab[:, :, :, ::-1],
-                in1=turn_t[:, angles, :].unsqueeze(1).to_broadcast([P, H, NI, 2]),
+                out=both[:, :, :, j % 2, :],
+                in0=banks[(span * 2 + t) * J + j][:].rearrange("p (h c) -> p h c", h=H).unsqueeze(1).to_broadcast([P, 2, H, HS]),
+                in1=factors[:, qt * J + j].unsqueeze(2).to_broadcast([P, 2, H, HS]),
                 op=MULT,
             )
 
         def rope_add(span, t, pair):
             if pair == 0:
                 new_chunk(span, t)
-            cos_prod, sin_prod = products_of[(span, t)]
+            both = products_of[(span, t)]
             engine = nc.vector if (span, t, pair) == (NSPAN - 1, K_, PAIRS - 1) else nc.gpsimd
             engine.tensor_tensor(
-                out=chunks[(span, t)][:, :, 2 * pair : 2 * pair + 2, :], in0=cos_prod[:], in1=sin_prod[:], op=ADD
+                out=chunks[(span, t)][:, :, 2 * pair : 2 * pair + 2, :].rearrange("p h j (i x) -> p h (j i) x", x=2),
+                in0=both[:, 0].rearrange("p h j (i x) -> p h (j i) x", x=2),
+                in1=both[:, 1].rearrange("p h j (i x) -> p h (j i) x", x=2)[:, :, :, ::-1],
+                op=ADD,
             )
 
         def v_slot(span, j):
@@ -246,23 +240,23 @@ def tile_causalselfattention2_pa_t_kernel(tc, x, w_attn, freqs_cos, freqs_sin, o
                 store_chunk(span, V_)
 
         def v_sum(span, two):
-            b, qt = divmod(span, NQ)
+            b = span // NQ
             v_turned = ps_vsum.tile([P, P], F32, name="v_turned")
             channels = slice(V_ * C + two * P, V_ * C + (two + 1) * P)
-            for j in range(J):
-                positions = slice((span * J + j) * P, (span * J + j + 1) * P)
+            for slot in range(SLOTS):
+                positions = slice((b * SLOTS + slot) * P, (b * SLOTS + slot + 1) * P)
                 nc.tensor.matmul_mx(
                     out=v_turned[:],
                     lhsT=w_codes[:, channels].bitcast(FP8X4),
                     lhsT_scale=w_scales[:, channels],
                     rhs=x_codes[:, positions].bitcast(FP8X4),
                     rhs_scale=x_scales[:, positions],
-                    start=(j == 0),
-                    stop=(j == J - 1),
+                    start=(slot == 0),
+                    stop=(slot == SLOTS - 1),
                 )
             waiting["reduces"].append(
                 lambda: nc.vector.tensor_reduce(
-                    out=v_sums[b][:, qt, two, :],
+                    out=v_sums[b][:, two, :],
                     in_=v_turned[:].rearrange("m (g n) -> m g n", g=G),
                     axis=LAST_AXIS,
                     op=ADD,
@@ -306,22 +300,22 @@ def tile_causalselfattention2_pa_t_kernel(tc, x, w_attn, freqs_cos, freqs_sin, o
 
         def store_means(b):
             do_reduces()
-            for qt in range(NQ):
-                nc.vector.tensor_tensor(
-                    out=group_sums[b][:, qt, V_, :, :].rearrange("m (a x) g -> m a x g", x=2),
-                    in0=v_sums[b][:, qt].unsqueeze(2).to_broadcast([P, H // 2, 2, G]),
-                    in1=own_half[:],
-                    op=MULT,
-                )
+            nc.vector.tensor_tensor(
+                out=group_sums[b][:, 0, V_, :, :].rearrange("m (a x) g -> m a x g", x=2),
+                in0=v_sums[b][:].unsqueeze(2).to_broadcast([P, H // 2, 2, G]),
+                in1=own_half[:],
+                op=MULT,
+            )
             means_ps = ps_words.tile([P, 3 * HS], F32, name="means_ps", tag="words")
             for t in range(3):
-                for qt in range(NQ):
+                parts = 1 if t == V_ else NQ
+                for qt in range(parts):
                     nc.tensor.matmul(
                         out=means_ps[:, t * HS : (t + 1) * HS],
                         lhsT=group_sums[b][:, qt, t, :, :].rearrange("m h g -> m (h g)"),
                         rhs=fold[:],
                         start=(qt == 0),
-                        stop=(qt == NQ - 1),
+                        stop=(qt == parts - 1),
                     )
             means = small.tile([P, 3 * HS], F32, name="means")
             nc.scalar.copy(out=means[:], in_=means_ps[:])
@@ -341,7 +335,7 @@ def tile_causalselfattention2_pa_t_kernel(tc, x, w_attn, freqs_cos, freqs_sin, o
                 t, pair = divmod(s, PAIRS)
                 if s == 0 and span % NQ == 0:
                     sums_qkv = small.tile([P, NQ, 3, H, G], F32, name="sums_qkv")
-                    sums_v = small.tile([P, NQ, H // 2, G], F32, name="sums_v")
+                    sums_v = small.tile([P, H // 2, G], F32, name="sums_v")
                     group_sums[span // NQ] = sums_qkv
                     v_sums[span // NQ] = sums_v
                 quantise_now = prepared["quantise"]
@@ -351,12 +345,12 @@ def tile_causalselfattention2_pa_t_kernel(tc, x, w_attn, freqs_cos, freqs_sin, o
                     operand = [("x", 0, 1), ("w", K_), ("w", V_), None, ("x", 1, 0), None, ("x", 1, 1), None][s]
                     whole = s < 2
                     v_now = [2 * (s - 4), 2 * (s - 4) + 1] if s >= 4 else []
-                    v_sums_now = [s - 4] if s >= 4 else []
+                    v_sums_now = []
                 else:
                     operand = ("x", span + 1, s // 4) if span + 1 < NSPAN and s % 4 == 0 else None
                     whole = False
                     v_now = [s]
-                    v_sums_now = [s // 2] if s % 2 == 1 else []
+                    v_sums_now = [s // 2] if s % 2 == 1 and span % NQ == NQ - 1 else []
                 if operand is not None:
                     sets, quantise = prepare_x(operand[1], operand[2]) if operand[0] == "x" else prepare_w(operand[1])
                     prepared["sets"] = sets

@@ -79,8 +79,8 @@ def tile_causalselfattention2_pa_t_kernel(tc, x, w_attn, freqs_cos, freqs_sin, o
         nc.sync.dma_start(out=cos_t[:], in_=freqs_cos.rearrange("(p j) i -> p (j i)", j=SLOTS))
         nc.sync.dma_start(out=sin_t[:], in_=freqs_sin.rearrange("(p j) i -> p (j i)", j=SLOTS))
         load_x(0, SETS, SETS)
-        load_w(K_ * SETS, SETS)
         load_w(V_ * SETS, SETS)
+        load_w(K_ * SETS, SETS)
         for span in range(1, NSPAN):
             load_x(span, 0, J)
         table_in = const.tile([P, 1], F32)
@@ -187,13 +187,18 @@ def tile_causalselfattention2_pa_t_kernel(tc, x, w_attn, freqs_cos, freqs_sin, o
         v_sums = {}
         waiting = {"reduces": []}
 
-        def store_chunk(span, t):
+        def store_slots(span, t, first, last):
             b, qt = divmod(span, NQ)
             for h in range(H):
                 nc.sync.dma_start(
-                    out=outs[t][b, h, :, 0:TG, :].rearrange("g (n j) c -> g n (j c)", j=SLOTS)[:, :, qt * J * HS : (qt + 1) * J * HS],
-                    in_=chunks[(span, t)][:, h, :, :].rearrange("p j c -> p (j c)"),
+                    out=outs[t][b, h, :, 0:TG, :].rearrange("g (n j) c -> g n (j c)", j=SLOTS)[:, :, (qt * J + first) * HS : (qt * J + last) * HS],
+                    in_=chunks[(span, t)][:, h, first:last, :].rearrange("p j c -> p (j c)"),
                 )
+
+        def store_when_due(span, t, done):
+            slots = J // 2 if span in (0, NSPAN - 1) else J
+            if done % slots == 0:
+                store_slots(span, t, done - slots, done)
 
         def new_chunk(span, t):
             chunk = chunk_pool.tile([P, H, J, HS], F32, name="chunk")
@@ -236,8 +241,7 @@ def tile_causalselfattention2_pa_t_kernel(tc, x, w_attn, freqs_cos, freqs_sin, o
             bank = ps_v.tile([P, C], F32, name="v_bank")
             mx_pass(bank[:], span, j, V_)
             nc.scalar.copy(out=chunks[(span, V_)][:, :, j, :], in_=bank[:].rearrange("p (h c) -> p h c", h=H))
-            if j == J - 1:
-                store_chunk(span, V_)
+            store_when_due(span, V_, j + 1)
 
         def v_sum(span, two):
             b = span // NQ
@@ -342,9 +346,9 @@ def tile_causalselfattention2_pa_t_kernel(tc, x, w_attn, freqs_cos, freqs_sin, o
                 prepared["quantise"] = None
                 two_sets = []
                 if span == 0:
-                    operand = [("x", 0, 1), ("w", K_), ("w", V_), None, ("x", 1, 0), None, ("x", 1, 1), None][s]
-                    whole = s < 2
-                    v_now = [2 * (s - 4), 2 * (s - 4) + 1] if s >= 4 else []
+                    operand = [("x", 0, 1), ("w", V_), ("w", K_), None, ("x", 1, 0), None, ("x", 1, 1), None][s]
+                    whole = s < 3
+                    v_now = [2 * (s - 2), 2 * (s - 2) + 1] if 2 <= s < 6 else []
                     v_sums_now = []
                 else:
                     operand = ("x", span + 1, s // 4) if span + 1 < NSPAN and s % 4 == 0 else None
@@ -385,5 +389,5 @@ def tile_causalselfattention2_pa_t_kernel(tc, x, w_attn, freqs_cos, freqs_sin, o
                 rope_add(span, t, pair)
             for call in side:
                 call()
-            if span < NSPAN and pair == PAIRS - 1:
-                store_chunk(span, t)
+            if span < NSPAN:
+                store_when_due(span, t, 2 * pair + 2)

@@ -19,6 +19,7 @@ NI = HS // 2
 TG = T // G
 SLOTS = T // P
 J = 8
+J_TILE = 4
 NQ = SLOTS // J
 NSPAN = B * NQ
 PAIRS = J // 2
@@ -43,7 +44,7 @@ def tile_causalselfattention2_pa_t_kernel(tc, x, w_attn, freqs_cos, freqs_sin, o
         x_pool = ctx.enter_context(tc.tile_pool(name="x_pool", bufs=NSPAN))
         stage = ctx.enter_context(tc.tile_pool(name="stage", bufs=2))
         products = ctx.enter_context(tc.tile_pool(name="products", bufs=5))
-        chunk_pool = ctx.enter_context(tc.tile_pool(name="chunk_pool", bufs=5))
+        chunk_pool = ctx.enter_context(tc.tile_pool(name="chunk_pool", bufs=11))
         small = ctx.enter_context(tc.tile_pool(name="small", bufs=2))
         ps_words = ctx.enter_context(tc.psum_pool(name="ps_words", bufs=1))
         ps_pass = ctx.enter_context(tc.psum_pool(name="ps_pass", bufs=3))
@@ -192,17 +193,19 @@ def tile_causalselfattention2_pa_t_kernel(tc, x, w_attn, freqs_cos, freqs_sin, o
             for h in range(H):
                 nc.sync.dma_start(
                     out=outs[t][b, h, :, 0:TG, :].rearrange("g (n j) c -> g n (j c)", j=SLOTS)[:, :, (qt * J + first) * HS : (qt * J + last) * HS],
-                    in_=chunks[(span, t)][:, h, first:last, :].rearrange("p j c -> p (j c)"),
+                    in_=chunks[(span, t, first // J_TILE)][:, h, :, :].rearrange("p j c -> p (j c)"),
                 )
 
         def store_when_due(span, t, done):
-            slots = J // 2 if span in (0, NSPAN - 1) else J
-            if done % slots == 0:
-                store_slots(span, t, done - slots, done)
+            if done % J_TILE == 0:
+                store_slots(span, t, done - J_TILE, done)
 
-        def new_chunk(span, t):
-            chunk = chunk_pool.tile([P, H, J, HS], F32, name="chunk")
-            chunks[(span, t)] = chunk
+        def chunk_slots(span, t, first, slots):
+            which = (span, t, first // J_TILE)
+            if first % J_TILE == 0 and which not in chunks:
+                chunk = chunk_pool.tile([P, H, J_TILE, HS], F32, name="chunk")
+                chunks[which] = chunk
+            return chunks[which][:, :, first % J_TILE : first % J_TILE + slots, :]
 
         def rope_pass(m):
             if m < NSPAN * 2 * J:
@@ -224,23 +227,19 @@ def tile_causalselfattention2_pa_t_kernel(tc, x, w_attn, freqs_cos, freqs_sin, o
             )
 
         def rope_add(span, t, pair):
-            if pair == 0:
-                new_chunk(span, t)
             both = products_of[(span, t)]
             engine = nc.vector if (span, t, pair) == (NSPAN - 1, K_, PAIRS - 1) else nc.gpsimd
             engine.tensor_tensor(
-                out=chunks[(span, t)][:, :, 2 * pair : 2 * pair + 2, :].rearrange("p h j (i x) -> p h (j i) x", x=2),
+                out=chunk_slots(span, t, 2 * pair, 2).rearrange("p h j (i x) -> p h (j i) x", x=2),
                 in0=both[:, 0].rearrange("p h j (i x) -> p h (j i) x", x=2),
                 in1=both[:, 1].rearrange("p h j (i x) -> p h (j i) x", x=2)[:, :, :, ::-1],
                 op=ADD,
             )
 
         def v_slot(span, j):
-            if j == 0:
-                new_chunk(span, V_)
             bank = ps_v.tile([P, C], F32, name="v_bank")
             mx_pass(bank[:], span, j, V_)
-            nc.scalar.copy(out=chunks[(span, V_)][:, :, j, :], in_=bank[:].rearrange("p (h c) -> p h c", h=H))
+            nc.scalar.copy(out=chunk_slots(span, V_, j, 1)[:, :, 0, :], in_=bank[:].rearrange("p (h c) -> p h c", h=H))
             store_when_due(span, V_, j + 1)
 
         def v_sum(span, two):
@@ -280,7 +279,7 @@ def tile_causalselfattention2_pa_t_kernel(tc, x, w_attn, freqs_cos, freqs_sin, o
                 for pair in range(PAIRS):
                     nc.tensor.matmul(
                         out=turned[:, h % HEADS_OF_TILE, :],
-                        lhsT=chunks[(span, t)][:, h, 2 * pair : 2 * pair + 2, :].rearrange("p j c -> p (j c)"),
+                        lhsT=chunk_slots(span, t, 2 * pair, 2)[:, h].rearrange("p j c -> p (j c)"),
                         rhs=ident[:],
                         is_transpose=True,
                         start=(pair == 0),

@@ -48,8 +48,7 @@ def tile_causalselfattention2_pa_t_kernel(tc, x, w_attn, freqs_cos, freqs_sin, o
         small = ctx.enter_context(tc.tile_pool(name="small", bufs=2))
         ps_words = ctx.enter_context(tc.psum_pool(name="ps_words", bufs=1))
         ps_pass = ctx.enter_context(tc.psum_pool(name="ps_pass", bufs=3))
-        ps_v = ctx.enter_context(tc.psum_pool(name="ps_v", bufs=1))
-        ps_vsum = ctx.enter_context(tc.psum_pool(name="ps_vsum", bufs=1))
+        ps_v = ctx.enter_context(tc.psum_pool(name="ps_v", bufs=2))
         ps_sums = ctx.enter_context(tc.psum_pool(name="ps_sums", bufs=2))
         ctx.enter_context(tc.manual_schedule())
 
@@ -237,14 +236,14 @@ def tile_causalselfattention2_pa_t_kernel(tc, x, w_attn, freqs_cos, freqs_sin, o
             )
 
         def v_slot(span, j):
-            bank = ps_v.tile([P, C], F32, name="v_bank")
+            bank = ps_v.tile([P, C], F32, name="v_bank", tag="v")
             mx_pass(bank[:], span, j, V_)
             nc.scalar.copy(out=chunk_slots(span, V_, j, 1)[:, :, 0, :], in_=bank[:].rearrange("p (h c) -> p h c", h=H))
             store_when_due(span, V_, j + 1)
 
         def v_sum(span, two):
             b = span // NQ
-            v_turned = ps_vsum.tile([P, P], F32, name="v_turned")
+            v_turned = ps_v.tile([P, P], F32, name="v_turned", tag="v")
             channels = slice(V_ * C + two * P, V_ * C + (two + 1) * P)
             for slot in range(SLOTS):
                 positions = slice((b * SLOTS + slot) * P, (b * SLOTS + slot + 1) * P)
@@ -266,30 +265,31 @@ def tile_causalselfattention2_pa_t_kernel(tc, x, w_attn, freqs_cos, freqs_sin, o
                 )
             )
 
-        def sum_step(n):
-            chunk_index, step = divmod(n, H // HEADS_OF_STEP)
-            span, t = divmod(chunk_index, 2)
-            b, qt = divmod(span, NQ)
+        def sum_step(span, t, part, step, pairs, in_tail=False):
+            b = span // NQ
             if step % 2 == 0:
-                turned = ps_sums.tile([P, HEADS_OF_TILE, P], F32, name="turned")
+                if in_tail:
+                    turned = ps_pass.tile([P, HEADS_OF_TILE, P], F32, name="turned", tag="bank")
+                else:
+                    turned = ps_sums.tile([P, HEADS_OF_TILE, P], F32, name="turned", tag="turned")
                 waiting["turned"] = turned
             turned = waiting["turned"]
             for i in range(HEADS_OF_STEP):
                 h = step * HEADS_OF_STEP + i
-                for pair in range(PAIRS):
+                for pair in pairs:
                     nc.tensor.matmul(
                         out=turned[:, h % HEADS_OF_TILE, :],
                         lhsT=chunk_slots(span, t, 2 * pair, 2)[:, h].rearrange("p j c -> p (j c)"),
                         rhs=ident[:],
                         is_transpose=True,
-                        start=(pair == 0),
-                        stop=(pair == PAIRS - 1),
+                        start=(pair == pairs[0]),
+                        stop=(pair == pairs[-1]),
                     )
             if step % 2 == 1:
                 first_head = (step // 2) * HEADS_OF_TILE
                 waiting["reduces"].append(
                     lambda: nc.vector.tensor_reduce(
-                        out=group_sums[b][:, qt, t, first_head : first_head + HEADS_OF_TILE, :],
+                        out=group_sums[b][:, part, t, first_head : first_head + HEADS_OF_TILE, :],
                         in_=turned[:].rearrange("m h (g n) -> m h g n", g=G),
                         axis=LAST_AXIS,
                         op=ADD,
@@ -311,7 +311,7 @@ def tile_causalselfattention2_pa_t_kernel(tc, x, w_attn, freqs_cos, freqs_sin, o
             )
             means_ps = ps_words.tile([P, 3 * HS], F32, name="means_ps", tag="words")
             for t in range(3):
-                parts = 1 if t == V_ else NQ
+                parts = {Q_: NQ, K_: NQ + (b == B - 1), V_: 1}[t]
                 for qt in range(parts):
                     nc.tensor.matmul(
                         out=means_ps[:, t * HS : (t + 1) * HS],
@@ -329,19 +329,33 @@ def tile_causalselfattention2_pa_t_kernel(tc, x, w_attn, freqs_cos, freqs_sin, o
                 )
 
         rope_pass(0)
-        sums_per_sequence = NQ * 2 * (H // HEADS_OF_STEP)
+        steps = H // HEADS_OF_STEP
+        sums_at = {}
+        for chunk_index in range(2 * NSPAN - 2):
+            for step in range(steps):
+                span, t = divmod(chunk_index, 2)
+                sums_at.setdefault(chunk_index * PAIRS + SUM_LAG + step, []).append((span, t, span % NQ, step, range(PAIRS)))
+        last_beat = NSPAN * BEATS - 1
+        for step in range(steps):
+            sums_at.setdefault(last_beat - 2 + step // 2, []).append((NSPAN - 1, Q_, NQ - 1, step, range(PAIRS)))
+        for step in range(steps):
+            sums_at.setdefault(last_beat, []).append((NSPAN - 1, K_, NQ - 1, step, range(PAIRS // 2)))
+        for step in range(steps):
+            sums_at.setdefault(last_beat + 1, []).append((NSPAN - 1, K_, NQ, step, range(PAIRS // 2, PAIRS), True))
+        means_at = {NQ * BEATS + SUM_LAG - 1: 0, last_beat + 1: B - 1}
         prepared = {"quantise": None, "sets": []}
-        for beat in range(NSPAN * BEATS + SUM_LAG):
+        for beat in range(NSPAN * BEATS + 1):
             span, s = divmod(beat, BEATS)
             side = []
             if span < NSPAN:
                 t, pair = divmod(s, PAIRS)
                 if s == 0 and span % NQ == 0:
-                    sums_qkv = small.tile([P, NQ, 3, H, G], F32, name="sums_qkv")
+                    sums_qkv = small.tile([P, NQ + 1, 3, H, G], F32, name="sums_qkv")
                     sums_v = small.tile([P, H // 2, G], F32, name="sums_v")
                     group_sums[span // NQ] = sums_qkv
                     v_sums[span // NQ] = sums_v
                 quantise_now = prepared["quantise"]
+                urgent = 0 if span == 0 and s in (1, 3) else 1
                 prepared["quantise"] = None
                 two_sets = []
                 if span == 0:
@@ -364,24 +378,24 @@ def tile_causalselfattention2_pa_t_kernel(tc, x, w_attn, freqs_cos, freqs_sin, o
                         prepared["sets"] = prepared["sets"][1:]
                         if not prepared["sets"]:
                             prepared["quantise"] = prepared["next"]
-                for j in v_now[0:1]:
-                    side.append(lambda j=j: v_slot(span, j))
-                side += two_sets
-                for j in v_now[1:]:
+                if span == 0:
+                    side += two_sets
+                for j in v_now:
                     side.append(lambda j=j: v_slot(span, j))
                 for two in v_sums_now:
                     side.append(lambda two=two: v_sum(span, two))
-            n = beat - SUM_LAG
-            if n >= 0:
-                side.append(lambda: sum_step(n))
-                if n % sums_per_sequence == sums_per_sequence - 1:
-                    side.append(lambda: store_means(n // sums_per_sequence))
+                if span > 0:
+                    side += two_sets
+            for work in sums_at.get(beat, []):
+                side.append(lambda work=work: sum_step(*work))
+            if beat in means_at:
+                side.append(lambda: store_means(means_at[beat]))
 
             if span < NSPAN:
                 for j in (2 * pair, 2 * pair + 1):
                     rope_pass((span * 2 + t) * J + j + 1)
                     rope_products(span, t, j)
-                    if j % 2 == 0 and quantise_now is not None:
+                    if j % 2 == urgent and quantise_now is not None:
                         quantise_now()
             do_reduces()
             if span < NSPAN:

from contextlib import ExitStack

import concourse.mybir as mybir
from concourse.masks import make_identity

F32 = mybir.dt.float32
BF16 = mybir.dt.bfloat16
U32 = mybir.dt.uint32
U8 = mybir.dt.uint8
FP8X4 = mybir.dt.float8_e4m3fn_x4
ADD = mybir.AluOpType.add
MULT = mybir.AluOpType.mult
LAST_AXIS = mybir.AxisListType.X

P = 128
B, T, C, H, G = 2, 2048, 512, 8, 16
HS = C // H
NI = HS // 2
TG = T // G
SLOTS = T // P
J = 8
J_TILE = 4
NQ = SLOTS // J
NSPAN = B * NQ
PAIRS = J // 2
WORDS = C // 2
PLANES = WORDS // P
PACK = 4
SETS = 4
PARTS = J // SETS
HEADS_OF_TILE = 4
HEADS_OF_STEP = 2
Q_, K_, V_ = 0, 1, 2
BEATS = 2 * PAIRS
SUM_LAG = 5
FLOPS = 2 * B * T * 3 * C * C


def tile_causalselfattention2_pa_t_kernel(tc, x, w_attn, freqs_cos, freqs_sin, out_0, out_1, out_2):
    nc = tc.nc
    outs = [out_0, out_1, out_2]
    with ExitStack() as ctx:
        const = ctx.enter_context(tc.tile_pool(name="const", bufs=1))
        x_pool = ctx.enter_context(tc.tile_pool(name="x_pool", bufs=NSPAN))
        stage = ctx.enter_context(tc.tile_pool(name="stage", bufs=2))
        products = ctx.enter_context(tc.tile_pool(name="products", bufs=5))
        chunk_pool = ctx.enter_context(tc.tile_pool(name="chunk_pool", bufs=11))
        small = ctx.enter_context(tc.tile_pool(name="small", bufs=2))
        ps_words = ctx.enter_context(tc.psum_pool(name="ps_words", bufs=1))
        ps_pass = ctx.enter_context(tc.psum_pool(name="ps_pass", bufs=3))
        ps_v = ctx.enter_context(tc.psum_pool(name="ps_v", bufs=2))
        ps_sums = ctx.enter_context(tc.psum_pool(name="ps_sums", bufs=2))
        ctx.enter_context(tc.manual_schedule())

        w_rows = const.tile([P, 3 * SETS, C], BF16)
        w_view = w_attn.rearrange("(r p) k -> p r k", p=P)
        x_rows = []
        for span in range(NSPAN):
            x_span = x_pool.tile([P, J * C], BF16, name="x_span")
            x_rows.append(x_span)

        def load_w(first, sets):
            nc.sync.dma_start(out=w_rows[:, first : first + sets, :], in_=w_view[:, first : first + sets, :])

        def load_x(span, first, slots):
            b, qt = divmod(span, NQ)
            view = x[b].rearrange("(p j) k -> p (j k)", j=SLOTS)
            columns = slice(first * C, (first + slots) * C)
            start = qt * J * C
            nc.sync.dma_start(out=x_rows[span][:, columns], in_=view[:, start + first * C : start + (first + slots) * C])

        load_w(0, 2)
        load_x(0, 0, 2)
        load_w(2, 2)
        load_x(0, 2, 2)

        cos_t = const.tile([P, SLOTS * NI], BF16)
        sin_t = const.tile([P, SLOTS * NI], BF16)
        nc.sync.dma_start(out=cos_t[:], in_=freqs_cos.rearrange("(p j) i -> p (j i)", j=SLOTS))
        nc.sync.dma_start(out=sin_t[:], in_=freqs_sin.rearrange("(p j) i -> p (j i)", j=SLOTS))
        load_x(0, SETS, SETS)
        load_w(V_ * SETS, SETS)
        load_w(K_ * SETS, SETS)
        for span in range(1, NSPAN):
            load_x(span, 0, J)
        table_in = const.tile([P, 1], F32)
        table_out = const.tile([P, 1], F32)
        nc.vector.memset(table_in[:], 0.0)
        nc.scalar.copy(out=table_out[:], in_=table_in[:])

        ident = const.tile([P, P], F32)
        make_identity(nc, ident[:])
        fold = const.tile([P, HS], F32)
        nc.vector.tensor_tensor(out=fold[:], in0=ident[:, 0:HS], in1=ident[:, HS:P], op=ADD)
        nc.vector.tensor_scalar_mul(out=fold[:], in0=fold[:], scalar1=1.0 / TG)
        own_half = const.tile([P, H // 2, 2, G], F32)
        nc.vector.memset(own_half[:], 1.0)
        nc.vector.memset(own_half[0:HS, :, 1, :], 0.0)
        nc.vector.memset(own_half[HS:P, :, 0, :], 0.0)
        sign = const.tile([P, 2, 2], F32)
        nc.gpsimd.memset(sign[:], 1.0)
        nc.gpsimd.memset(sign[:, 1, 1:2], -1.0)
        factors = const.tile([P, SLOTS, 2, HS], BF16)
        for first in (0, J):
            for which, table in enumerate((cos_t, sin_t)):
                nc.gpsimd.tensor_tensor(
                    out=factors[:, first : first + J, which, :].rearrange("p s (i x) -> p s i x", x=2),
                    in0=table[:, first * NI : (first + J) * NI].rearrange("p (s i) -> p s i", s=J).unsqueeze(3).to_broadcast([P, J, NI, 2]),
                    in1=sign[:, which, :].unsqueeze(1).unsqueeze(1).to_broadcast([P, J, NI, 2]),
                    op=MULT,
                )

        w_codes = const.tile([P, 3 * C], U32, align_bytes=64)
        w_scales = const.tile([P, 3 * C], U8, align_bytes=64)
        x_codes = const.tile([P, NSPAN * J * P], U32, align_bytes=64)
        x_scales = const.tile([P, NSPAN * J * P], U8, align_bytes=64)
        w_words = w_rows[:].bitcast(F32)

        def prepare(words, matrix, columns, codes, scales, in_head, copy):
            grouped = stage.tile([P, SETS * P * PACK], BF16, align_bytes=64, name="grouped")
            grouped_words = grouped[:].bitcast(F32).rearrange("q (s m u) -> q s m u", s=SETS, u=PLANES)

            def transpose_two(s):
                if in_head:
                    planes = ps_pass.tile([P, 2, PLANES, P], F32, name="planes", tag="bank")
                else:
                    planes = ps_words.tile([P, 2, PLANES, P], F32, name="planes", tag="words")
                for i in range(2):
                    for u in range(PLANES):
                        nc.tensor.transpose(out=planes[:, i, u, :], in_=words(s + i, u), identity=matrix[:])
                copy(out=grouped_words[:, s : s + 2], in_=planes[:].rearrange("q s u m -> q s m u"))

            def quantise():
                nc.vector.quantize_mx(out=codes[:, columns].bitcast(FP8X4), scales=scales[:, columns], in_=grouped[:])

            return [lambda s=s: transpose_two(s) for s in range(0, SETS, 2)], quantise

        def prepare_w(t, in_head=False):
            return prepare(
                lambda s, u: w_words[:, SETS * t + s, u::PLANES],
                ident,
                slice(t * C, (t + 1) * C),
                w_codes,
                w_scales,
                in_head,
                nc.scalar.copy,
            )

        def prepare_x(span, part, in_head=False):
            x_words = x_rows[span][:].bitcast(F32)
            first = (span * J + part * SETS) * P
            return prepare(
                lambda s, u: x_words[:, (part * SETS + s) * WORDS + u : (part * SETS + s + 1) * WORDS : PLANES],
                ident,
                slice(first, first + SETS * P),
                x_codes,
                x_scales,
                in_head,
                nc.vector.tensor_copy if in_head else nc.scalar.copy,
            )

        def mx_pass(out, span, j, t):
            positions = slice((span * J + j) * P, (span * J + j + 1) * P)
            channels = slice(t * C, (t + 1) * C)
            nc.tensor.matmul_mx(
                out=out,
                lhsT=x_codes[:, positions].bitcast(FP8X4),
                lhsT_scale=x_scales[:, positions],
                rhs=w_codes[:, channels].bitcast(FP8X4),
                rhs_scale=w_scales[:, channels],
                start=True,
                stop=True,
            )

        sets_w, quantise_w = prepare_w(Q_, in_head=True)
        sets_x, quantise_x = prepare_x(0, 0, in_head=True)
        for call_w, call_x in zip(sets_w, sets_x):
            call_w()
            call_x()
        quantise_w()
        quantise_x()

        chunks = {}
        products_of = {}
        banks = {}
        group_sums = {}
        v_sums = {}
        waiting = {"reduces": []}

        def store_slots(span, t, first, last):
            b, qt = divmod(span, NQ)
            for h in range(H):
                nc.sync.dma_start(
                    out=outs[t][b, h, :, 0:TG, :].rearrange("g (n j) c -> g n (j c)", j=SLOTS)[:, :, (qt * J + first) * HS : (qt * J + last) * HS],
                    in_=chunks[(span, t, first // J_TILE)][:, h, :, :].rearrange("p j c -> p (j c)"),
                )

        def store_when_due(span, t, done):
            if done % J_TILE == 0:
                store_slots(span, t, done - J_TILE, done)

        def chunk_slots(span, t, first, slots):
            which = (span, t, first // J_TILE)
            if first % J_TILE == 0 and which not in chunks:
                chunk = chunk_pool.tile([P, H, J_TILE, HS], F32, name="chunk")
                chunks[which] = chunk
            return chunks[which][:, :, first % J_TILE : first % J_TILE + slots, :]

        def rope_pass(m):
            if m < NSPAN * 2 * J:
                bank = ps_pass.tile([P, C], F32, name="bank", tag="bank")
                mx_pass(bank[:], m // (2 * J), m % J, m // J % 2)
                banks[m] = bank

        def rope_products(span, t, j):
            qt = span % NQ
            if j % 2 == 0:
                both = products.tile([P, 2, H, 2, HS], F32, name="both")
                products_of[(span, t)] = both
            both = products_of[(span, t)]
            nc.vector.tensor_tensor(
                out=both[:, :, :, j % 2, :],
                in0=banks[(span * 2 + t) * J + j][:].rearrange("p (h c) -> p h c", h=H).unsqueeze(1).to_broadcast([P, 2, H, HS]),
                in1=factors[:, qt * J + j].unsqueeze(2).to_broadcast([P, 2, H, HS]),
                op=MULT,
            )

        def rope_add(span, t, pair):
            both = products_of[(span, t)]
            engine = nc.vector if (span, t, pair) == (NSPAN - 1, K_, PAIRS - 1) else nc.gpsimd
            engine.tensor_tensor(
                out=chunk_slots(span, t, 2 * pair, 2).rearrange("p h j (i x) -> p h (j i) x", x=2),
                in0=both[:, 0].rearrange("p h j (i x) -> p h (j i) x", x=2),
                in1=both[:, 1].rearrange("p h j (i x) -> p h (j i) x", x=2)[:, :, :, ::-1],
                op=ADD,
            )

        def v_slot(span, j):
            bank = ps_v.tile([P, C], F32, name="v_bank", tag="v")
            mx_pass(bank[:], span, j, V_)
            nc.scalar.copy(out=chunk_slots(span, V_, j, 1)[:, :, 0, :], in_=bank[:].rearrange("p (h c) -> p h c", h=H))
            store_when_due(span, V_, j + 1)

        def v_sum(span, two):
            b = span // NQ
            v_turned = ps_v.tile([P, P], F32, name="v_turned", tag="v")
            channels = slice(V_ * C + two * P, V_ * C + (two + 1) * P)
            for slot in range(SLOTS):
                positions = slice((b * SLOTS + slot) * P, (b * SLOTS + slot + 1) * P)
                nc.tensor.matmul_mx(
                    out=v_turned[:],
                    lhsT=w_codes[:, channels].bitcast(FP8X4),
                    lhsT_scale=w_scales[:, channels],
                    rhs=x_codes[:, positions].bitcast(FP8X4),
                    rhs_scale=x_scales[:, positions],
                    start=(slot == 0),
                    stop=(slot == SLOTS - 1),
                )
            waiting["reduces"].append(
                lambda: nc.vector.tensor_reduce(
                    out=v_sums[b][:, two, :],
                    in_=v_turned[:].rearrange("m (g n) -> m g n", g=G),
                    axis=LAST_AXIS,
                    op=ADD,
                )
            )

        def sum_step(span, t, part, step, pairs, in_tail=False):
            b = span // NQ
            if step % 2 == 0:
                if in_tail:
                    turned = ps_pass.tile([P, HEADS_OF_TILE, P], F32, name="turned", tag="bank")
                else:
                    turned = ps_sums.tile([P, HEADS_OF_TILE, P], F32, name="turned", tag="turned")
                waiting["turned"] = turned
            turned = waiting["turned"]
            for i in range(HEADS_OF_STEP):
                h = step * HEADS_OF_STEP + i
                for pair in pairs:
                    nc.tensor.matmul(
                        out=turned[:, h % HEADS_OF_TILE, :],
                        lhsT=chunk_slots(span, t, 2 * pair, 2)[:, h].rearrange("p j c -> p (j c)"),
                        rhs=ident[:],
                        is_transpose=True,
                        start=(pair == pairs[0]),
                        stop=(pair == pairs[-1]),
                    )
            if step % 2 == 1:
                first_head = (step // 2) * HEADS_OF_TILE
                waiting["reduces"].append(
                    lambda: nc.vector.tensor_reduce(
                        out=group_sums[b][:, part, t, first_head : first_head + HEADS_OF_TILE, :],
                        in_=turned[:].rearrange("m h (g n) -> m h g n", g=G),
                        axis=LAST_AXIS,
                        op=ADD,
                    )
                )

        def do_reduces():
            for call in waiting["reduces"]:
                call()
            waiting["reduces"] = []

        def store_means(b):
            do_reduces()
            nc.vector.tensor_tensor(
                out=group_sums[b][:, 0, V_, :, :].rearrange("m (a x) g -> m a x g", x=2),
                in0=v_sums[b][:].unsqueeze(2).to_broadcast([P, H // 2, 2, G]),
                in1=own_half[:],
                op=MULT,
            )
            means_ps = ps_words.tile([P, 3 * HS], F32, name="means_ps", tag="words")
            for t in range(3):
                parts = {Q_: NQ, K_: NQ + (b == B - 1), V_: 1}[t]
                for qt in range(parts):
                    nc.tensor.matmul(
                        out=means_ps[:, t * HS : (t + 1) * HS],
                        lhsT=group_sums[b][:, qt, t, :, :].rearrange("m h g -> m (h g)"),
                        rhs=fold[:],
                        start=(qt == 0),
                        stop=(qt == parts - 1),
                    )
            means = small.tile([P, 3 * HS], F32, name="means")
            nc.scalar.copy(out=means[:], in_=means_ps[:])
            for t in range(3):
                nc.sync.dma_start(
                    out=outs[t][b, :, :, TG, :].rearrange("h g c -> (h g) c"),
                    in_=means[:, t * HS : (t + 1) * HS],
                )

        rope_pass(0)
        steps = H // HEADS_OF_STEP
        sums_at = {}
        for chunk_index in range(2 * NSPAN - 2):
            for step in range(steps):
                span, t = divmod(chunk_index, 2)
                sums_at.setdefault(chunk_index * PAIRS + SUM_LAG + step, []).append((span, t, span % NQ, step, range(PAIRS)))
        last_beat = NSPAN * BEATS - 1
        for step in range(steps):
            sums_at.setdefault(last_beat - 2 + step // 2, []).append((NSPAN - 1, Q_, NQ - 1, step, range(PAIRS)))
        for step in range(steps):
            sums_at.setdefault(last_beat, []).append((NSPAN - 1, K_, NQ - 1, step, range(PAIRS // 2)))
        for step in range(steps):
            sums_at.setdefault(last_beat + 1, []).append((NSPAN - 1, K_, NQ, step, range(PAIRS // 2, PAIRS), True))
        means_at = {NQ * BEATS + SUM_LAG - 1: 0, last_beat + 1: B - 1}
        prepared = {"quantise": None, "sets": []}
        for beat in range(NSPAN * BEATS + 1):
            span, s = divmod(beat, BEATS)
            side = []
            if span < NSPAN:
                t, pair = divmod(s, PAIRS)
                if s == 0 and span % NQ == 0:
                    sums_qkv = small.tile([P, NQ + 1, 3, H, G], F32, name="sums_qkv")
                    sums_v = small.tile([P, H // 2, G], F32, name="sums_v")
                    group_sums[span // NQ] = sums_qkv
                    v_sums[span // NQ] = sums_v
                quantise_now = prepared["quantise"]
                urgent = 0 if span == 0 and s in (1, 3) else 1
                prepared["quantise"] = None
                two_sets = []
                if span == 0:
                    operand = [("x", 0, 1), ("w", V_), ("w", K_), None, ("x", 1, 0), None, ("x", 1, 1), None][s]
                    whole = s < 3
                    v_now = [2 * (s - 2), 2 * (s - 2) + 1] if 2 <= s < 6 else []
                    v_sums_now = []
                else:
                    operand = ("x", span + 1, s // 4) if span + 1 < NSPAN and s % 4 == 0 else None
                    whole = False
                    v_now = [s]
                    v_sums_now = [s // 2] if s % 2 == 1 and span % NQ == NQ - 1 else []
                if operand is not None:
                    sets, quantise = prepare_x(operand[1], operand[2]) if operand[0] == "x" else prepare_w(operand[1])
                    prepared["sets"] = sets
                    prepared["next"] = quantise
                for i in range(2 if whole else 1):
                    if prepared["sets"]:
                        two_sets.append(prepared["sets"][0])
                        prepared["sets"] = prepared["sets"][1:]
                        if not prepared["sets"]:
                            prepared["quantise"] = prepared["next"]
                if span == 0:
                    side += two_sets
                for j in v_now:
                    side.append(lambda j=j: v_slot(span, j))
                for two in v_sums_now:
                    side.append(lambda two=two: v_sum(span, two))
                if span > 0:
                    side += two_sets
            for work in sums_at.get(beat, []):
                side.append(lambda work=work: sum_step(*work))
            if beat in means_at:
                side.append(lambda: store_means(means_at[beat]))

            if span < NSPAN:
                for j in (2 * pair, 2 * pair + 1):
                    rope_pass((span * 2 + t) * J + j + 1)
                    rope_products(span, t, j)
                    if j % 2 == urgent and quantise_now is not None:
                        quantise_now()
            do_reduces()
            if span < NSPAN:
                rope_add(span, t, pair)
            for call in side:
                call()
            if span < NSPAN:
                store_when_due(span, t, 2 * pair + 2)
